import numpy as np
import ml_dtypes


def mxq(x, axis, fmt="e4m3"):
    dtype, down = {"e4m3": (ml_dtypes.float8_e4m3fn, 7), "e5m2": (ml_dtypes.float8_e5m2, 14)}[fmt]
    v = np.moveaxis(np.asarray(x, np.float32).astype(ml_dtypes.bfloat16).astype(np.float64), axis, -1)
    blocks = v.reshape(v.shape[:-1] + (-1, 32))
    amax = np.abs(blocks).max(-1, keepdims=True)
    byte = np.maximum(np.where(amax > 0, np.frexp(amax)[1] - 1 + 127, 0) - down, 1)
    scale = np.exp2(byte - 127.0)
    codes = (blocks / scale).astype(np.float32).astype(dtype).astype(np.float64)
    return np.moveaxis((codes * scale).reshape(v.shape), -1, axis)


WIDE = False


def mx_kscale(k):
    if not WIDE:
        return np.ones(k)
    levels = np.array([10, -10, 5, -5, 0])
    if k % 512:
        return np.exp2(np.random.permutation(np.resize(levels, k // 32))).repeat(32)
    a = np.empty((k // 512, 16))
    for p in range(k // 512):
        a[p, :8] = np.random.permutation(np.resize(levels, 8))
        for g in range(8):
            far = levels[np.abs(levels - a[p, g]) >= 10]
            a[p, g + 8] = far[np.random.randint(len(far))]
    return np.exp2(a.ravel()).repeat(32)


BF16 = ml_dtypes.bfloat16


def bf(x):
    return np.asarray(x, np.float32).astype(BF16)


def f64(x):
    return np.asarray(x).astype(np.float64)


B, K, M, D = 8192, 128, 4, 512
KM = K * M
SX = 1.2 / D ** 0.25
TINY = 1e-10


def softmax(v, axis):
    e = np.exp(v - v.max(axis, keepdims=True))
    return e / e.sum(axis, keepdims=True)


def setup_inputs():
    s = mx_kscale(D)
    return {"x": bf(np.random.standard_normal((B, D)) * SX * s),
            "gamma_class": bf(softmax(2.0 * np.random.standard_normal((B, K)), 1)),
            "mu": bf(np.random.standard_normal((K, M, D)) * SX * s),
            "cur_var": bf(np.random.uniform(0.8, 1.2, (K, M, D)) * s * s),
            "pi": bf((0.5 + np.random.random((K, M))) / M)}


def reference(x, gamma_class, mu, cur_var, pi):
    x = f64(x)
    mu = f64(mu).reshape(KM, D)
    cur_var = f64(cur_var).reshape(KM, D)
    inv_var = 1.0 / cur_var
    maha = ((mxq(x * x, 1, "e4m3") @ mxq(inv_var, 1, "e4m3").T)
            - 2.0 * (mxq(x, 1, "e4m3") @ mxq(mu * inv_var, 1, "e4m3").T)
            + np.sum(mu * mu * inv_var, axis=-1)[None])
    log_det = np.sum(np.log(cur_var), axis=-1)
    log_lik = -0.5 * (log_det[None] + maha)
    log_joint = (np.log(f64(pi) + TINY).reshape(KM)[None] + log_lik).reshape(B, K, M)
    top = log_joint.max(2, keepdims=True)
    lse = top + np.log(np.exp(log_joint - top).sum(2, keepdims=True))
    log_r = log_joint - lse
    return f64(gamma_class)[:, :, None] * np.exp(log_r)

@@ -1,0 +1,394 @@
+from contextlib import ExitStack
+
+import concourse.mybir as mybir
+from concourse.masks import make_identity
+
+F32 = mybir.dt.float32
+BF16 = mybir.dt.bfloat16
+U32 = mybir.dt.uint32
+U8 = mybir.dt.uint8
+FP8X4 = mybir.dt.float8_e4m3fn_x4
+ALU = mybir.AluOpType
+ACT = mybir.ActivationFunctionType
+
+P = 128
+SAMPLES = 8192
+CLASSES = 128
+MODES = 4
+FEATURES = 512
+PACK = 4
+TILES = SAMPLES // P
+TILES_PER_BLOCK = 4
+BLOCKS = TILES // TILES_PER_BLOCK
+BLOCK = TILES_PER_BLOCK * P
+HALF = BLOCK // 2
+GAMMA_LOADS = 4
+FLOPS = 2 * 2 * SAMPLES * CLASSES * MODES * FEATURES
+
+AHEAD = 3
+GROUP = 4
+LN_DELAY = 2
+LAG = (GROUP - 1) + LN_DELAY + 2
+
+WEIGHT_BANKS = ("et0", "et1", "rt", "p1", "p2", "p3")
+DRAIN_BANKS = ("p1", "p2", "p3", "xt0", "xt1", "et0", "et1")
+FIRST_DRAIN_TILE = TILES_PER_BLOCK * (BLOCKS - LAG) + 2
+
+
+def tile_dota_mix_pa_t_kernel(tc, x, gamma_class, mu, cur_var, pi, out):
+    nc = tc.nc
+    x_rows = x.rearrange("(p j) d -> p j d", j=TILES)
+    gamma_rows = gamma_class.rearrange("(p j) k -> p j k", j=TILES)
+    out_rows = out.rearrange("(p j) k m -> p j (k m)", j=TILES)
+
+    with ExitStack() as ctx:
+        ctx.enter_context(tc.manual_schedule())
+        const = ctx.enter_context(tc.tile_pool(name="const", bufs=1))
+        xin = ctx.enter_context(tc.tile_pool(name="xin", bufs=4))
+        grp = ctx.enter_context(tc.tile_pool(name="grp", bufs=3))
+        cod = ctx.enter_context(tc.tile_pool(name="cod", bufs=3))
+        two = ctx.enter_context(tc.tile_pool(name="two", bufs=2))
+        tops = ctx.enter_context(tc.tile_pool(name="tops", bufs=4))
+        sums = ctx.enter_context(tc.tile_pool(name="sums", bufs=LAG + 1))
+        outp = ctx.enter_context(tc.tile_pool(name="outp", bufs=3))
+        psum = ctx.enter_context(tc.psum_pool(name="psum", bufs=1))
+
+        identity = const.tile([P, P], F32, name="identf")
+        w_words = const.tile([P, 2, MODES, CLASSES], U32, name="wq", align_bytes=64)
+        w_scales = const.tile([P, 2, MODES, CLASSES], U8, name="ws", align_bytes=64)
+        dbias = const.tile([P, MODES], F32, name="bd")
+        gamma_sb = const.tile([P, TILES, CLASSES], BF16, name="g_sb")
+
+        x_sb = {}
+        x_t = {}
+        x_grouped = {}
+        xx_grouped = {}
+        operands = {}
+        group_acc = {}
+        top = {}
+        expo = {}
+        esum = {}
+        rsum_t = {}
+        ratio = {}
+        expo_t = {}
+        result = {}
+
+        def is_block(i):
+            return 0 <= i < BLOCKS
+
+
+        def load_x(i):
+            x_sb[i] = xin.tile([P, TILES_PER_BLOCK, FEATURES], BF16, name="x_sb")
+            nc.sync.dma_start(out=x_sb[i][:], in_=x_rows[:, i * TILES_PER_BLOCK : (i + 1) * TILES_PER_BLOCK, :])
+
+        def load_gamma(c):
+            js = slice(c * TILES // GAMMA_LOADS, (c + 1) * TILES // GAMMA_LOADS)
+            nc.sync.dma_start(out=gamma_sb[:, js, :], in_=gamma_rows[:, js, :])
+
+        def transpose_x(i, h):
+            x_t[(i, h)] = psum.tile([P, 2, HALF], F32, tag="xt%d" % h, name="xt")
+            pairs = x_sb[i][:].bitcast(F32)
+            for jj in range(2):
+                for u in range(2):
+                    nc.tensor.transpose(
+                        x_t[(i, h)][:, u, jj * P : (jj + 1) * P], pairs[:, 2 * h + jj, u : 2 * P : 2], identity[:]
+                    )
+
+        def copy_x(i, h, on_vector):
+            if h == 0:
+                x_grouped[i] = grp.tile([P, BLOCK, PACK], BF16, name="xg", align_bytes=64)
+                xx_grouped[i] = grp.tile([P, BLOCK, PACK], BF16, name="x2g", align_bytes=64)
+            cols = slice(h * HALF, (h + 1) * HALF)
+            dst = x_grouped[i][:].bitcast(F32)[:, cols, :]
+            src = x_t[(i, h)][:].rearrange("p u c -> p c u")
+            if on_vector:
+                nc.vector.tensor_copy(out=dst, in_=src)
+            else:
+                nc.scalar.copy(out=dst, in_=src)
+
+        def square_x(i, h):
+            cols = slice(h * HALF, (h + 1) * HALF)
+            nc.scalar.activation(
+                out=xx_grouped[i][:, cols, :].rearrange("p c (u e) -> p c u e", e=2),
+                in_=x_t[(i, h)][:].bitcast(BF16).rearrange("p u (c e) -> p c u e", e=2),
+                func=ACT.Square,
+            )
+
+        def copy_and_square_x(i):
+            for h in range(2):
+                copy_x(i, h, False)
+                square_x(i, h)
+
+        def quantise_x(i):
+            x_words = cod.tile([P, BLOCK], U32, name="xq", align_bytes=64)
+            x_scales = cod.tile([P, BLOCK], U8, name="xs", align_bytes=64)
+            xx_words = cod.tile([P, BLOCK], U32, name="x2q", align_bytes=64)
+            xx_scales = cod.tile([P, BLOCK], U8, name="x2s", align_bytes=64)
+            operands[i] = ((xx_words, xx_scales), (x_words, x_scales))
+            nc.vector.quantize_mx(
+                out=x_words[:].bitcast(FP8X4), scales=x_scales[:], in_=x_grouped[i][:].rearrange("p c t -> p (c t)")
+            )
+
+        def quantise_xx(i):
+            xx_words, xx_scales = operands[i][0]
+            nc.vector.quantize_mx(
+                out=xx_words[:].bitcast(FP8X4), scales=xx_scales[:], in_=xx_grouped[i][:].rearrange("p c t -> p (c t)")
+            )
+
+
+        def mx_group(i, m):
+            group_acc[(i, m)] = psum.tile([P, BLOCK], F32, tag="p%d" % m, name="acc")
+            passes = ((0, m), (0, 0), (1, m), (1, 0))
+            for n, (w, mode) in enumerate(passes):
+                words, scales = operands[i][w]
+                nc.tensor.matmul_mx(
+                    out=group_acc[(i, m)][:],
+                    lhsT=w_words[:, w, mode, :].bitcast(FP8X4),
+                    lhsT_scale=w_scales[:, w, mode, :],
+                    rhs=words[:].bitcast(FP8X4),
+                    rhs_scale=scales[:],
+                    start=(n == 0),
+                    stop=(n == len(passes) - 1),
+                )
+
+        def running_max(i, m):
+            if m == 1:
+                top[i] = tops.tile([P, BLOCK], F32, name="top")
+                nc.vector.tensor_scalar(
+                    out=top[i][:], in0=group_acc[(i, 1)][:], scalar1=dbias[:, 1:2], scalar2=0.0, op0=ALU.add, op1=ALU.max
+                )
+            else:
+                nc.vector.scalar_tensor_tensor(
+                    out=top[i][:],
+                    in0=group_acc[(i, m)][:],
+                    scalar=dbias[:, m : m + 1],
+                    in1=top[i][:],
+                    op0=ALU.add,
+                    op1=ALU.max,
+                )
+
+        def subtract_max(i, m):
+            if m == 1:
+                expo[i] = big.tile([P, MODES, BLOCK], F32, name="de")
+            nc.vector.scalar_tensor_tensor(
+                out=expo[i][:, m, :],
+                in0=group_acc[(i, m)][:],
+                scalar=dbias[:, m : m + 1],
+                in1=top[i][:],
+                op0=ALU.add,
+                op1=ALU.subtract,
+            )
+
+        def exponentials(i):
+            nc.scalar.activation(out=expo[i][:, 0, :], in_=top[i][:], func=ACT.Exp, scale=-1.0)
+            nc.scalar.activation(out=expo[i][:, 1:4, :], in_=expo[i][:, 1:4, :], func=ACT.Exp)
+
+        def sum_modes(i):
+            half_sums = two.tile([P, 2, BLOCK], F32, name="hs")
+            nc.gpsimd.tensor_tensor(out=half_sums[:], in0=expo[i][:, 0:2, :], in1=expo[i][:, 2:4, :], op=ALU.add)
+            esum[i] = sums.tile([P, BLOCK], F32, name="ssum")
+            nc.gpsimd.tensor_tensor(out=esum[i][:], in0=half_sums[:, 0, :], in1=half_sums[:, 1, :], op=ALU.add)
+
+        def reciprocal_sums(first):
+            for i in range(first, first + GROUP):
+                nc.scalar.activation(out=esum[i][:], in_=esum[i][:], func=ACT.Ln)
+            for i in range(first, first + GROUP):
+                nc.scalar.activation(out=esum[i][:], in_=esum[i][:], func=ACT.Exp, scale=-1.0)
+
+
+        def transpose_rsum(i):
+            rsum_t[i] = psum.tile([P, TILES_PER_BLOCK, CLASSES], F32, tag="rt", name="rt")
+            for jl in range(TILES_PER_BLOCK):
+                nc.tensor.transpose(rsum_t[i][:, jl, :], esum[i][:, jl * P : (jl + 1) * P], identity[:])
+
+        def times_gamma(i):
+            ratio[i] = two.tile([P, TILES_PER_BLOCK, CLASSES], F32, name="rr")
+            js = slice(i * TILES_PER_BLOCK, (i + 1) * TILES_PER_BLOCK)
+            nc.vector.tensor_tensor(out=ratio[i][:], in0=rsum_t[i][:], in1=gamma_sb[:, js, :], op=ALU.mult)
+            result[i] = outp.tile([P, TILES_PER_BLOCK, CLASSES * MODES], F32, name="o_sb")
+
+        def transpose_expo(i, jl):
+            drained = TILES_PER_BLOCK * i + jl - FIRST_DRAIN_TILE
+            bank = DRAIN_BANKS[drained % len(DRAIN_BANKS)] if drained >= 0 else "et%d" % (jl % 2)
+            expo_t[(i, jl)] = psum.tile([P, MODES, CLASSES], F32, tag=bank, name="et")
+            for m in range(MODES):
+                nc.tensor.transpose(expo_t[(i, jl)][:, m, :], expo[i][:, m, jl * P : (jl + 1) * P], identity[:])
+
+        def finish_tile(i, jl):
+            nc.vector.tensor_tensor(
+                out=result[i][:, jl, :].rearrange("p (k m) -> p k m", m=MODES),
+                in0=expo_t[(i, jl)][:].rearrange("p m k -> p k m"),
+                in1=ratio[i][:, jl, :].unsqueeze(2).to_broadcast([P, CLASSES, MODES]),
+                op=ALU.mult,
+            )
+            nc.sync.dma_start(out=out_rows[:, i * TILES_PER_BLOCK + jl, :], in_=result[i][:, jl, :])
+
+        with tc.tile_pool(name="prep", bufs=1) as prep:
+            var_sb = prep.tile([P, MODES, FEATURES], BF16, name="var_sb")
+            mu_sb = prep.tile([P, MODES, FEATURES], BF16, name="mu_sb")
+            pi_sb = prep.tile([P, MODES], BF16, name="pi_sb")
+            nc.scalar.dma_start(out=pi_sb[:], in_=pi)
+            for m in range(MODES):
+                nc.sync.dma_start(out=var_sb[:, m, :], in_=cur_var[:, m, :])
+            load_x(0)
+            nc.sync.dma_start(out=mu_sb[:], in_=mu)
+            for i in range(1, AHEAD + 1):
+                load_x(i)
+            make_identity(nc, identity[:])
+
+            ln_var = prep.tile([P, MODES, FEATURES], F32, name="lnv")
+            seed = prep.tile([P, MODES, PACK, P], F32, name="y0p")
+            neg_iv = prep.tile([P, MODES, PACK, P], F32, name="nivp")
+            neg_mu_iv = prep.tile([P, MODES, PACK, P], F32, name="nmivp")
+            neg_mu2_iv = prep.tile([P, MODES, PACK, P], F32, name="tmp")
+            w_grouped = prep.tile([P, 2, MODES, CLASSES * PACK], BF16, name="wg", align_bytes=64)
+            log_det = prep.tile([P, MODES], F32, name="ld")
+            pi_eps = prep.tile([P, MODES], F32, name="pif")
+            ln_pi = prep.tile([P, MODES], F32, name="lnpi")
+            neg_quad = prep.tile([P, MODES], F32, name="qs")
+            bias = prep.tile([P, MODES], F32, name="bias")
+            w_t = {}
+
+            def by_value(ap):
+                return ap.rearrange("k (q t) -> k t q", t=PACK)
+
+            def split(ap):
+                return ap
+
+            def flat(ap):
+                return ap.rearrange("k t q -> k (t q)")
+
+            nc.gpsimd.tensor_scalar(out=pi_eps[:], in0=pi_sb[:], scalar1=1e-10, scalar2=0.0, op0=ALU.add, op1=ALU.add)
+            for m in range(MODES):
+                nc.scalar.activation(
+                    out=ln_var[:, m, :], in_=var_sb[:, m, :], func=ACT.Ln, accum_out=log_det[:, m : m + 1]
+                )
+            nc.scalar.activation(out=ln_pi[:], in_=pi_eps[:], func=ACT.Ln)
+
+            for h in range(2):
+                transpose_x(0, h)
+            for h in range(2):
+                copy_x(0, h, True)
+            quantise_x(0)
+
+            for m in range(MODES):
+                nc.scalar.activation(out=split(seed[:, m, :, :]), in_=by_value(ln_var[:, m, :]), func=ACT.Exp, scale=-1.0)
+            for h in range(2):
+                square_x(0, h)
+            for h in range(2):
+                transpose_x(1, h)
+
+            for m in range(MODES):
+                nc.vector.tensor_tensor(
+                    out=split(neg_iv[:, m, :, :]), in0=by_value(var_sb[:, m, :]), in1=split(seed[:, m, :, :]), op=ALU.mult
+                )
+                nc.vector.scalar_tensor_tensor(
+                    out=flat(neg_iv[:, m, :, :]),
+                    in0=flat(neg_iv[:, m, :, :]),
+                    scalar=2.0,
+                    in1=flat(seed[:, m, :, :]),
+                    op0=ALU.subtract,
+                    op1=ALU.mult,
+                )
+                nc.vector.tensor_tensor(
+                    out=split(neg_mu_iv[:, m, :, :]), in0=by_value(mu_sb[:, m, :]), in1=split(neg_iv[:, m, :, :]), op=ALU.mult
+                )
+                nc.gpsimd.tensor_tensor(
+                    out=split(neg_mu2_iv[:, m, :, :]),
+                    in0=by_value(mu_sb[:, m, :]),
+                    in1=split(neg_mu_iv[:, m, :, :]),
+                    op=ALU.mult,
+                )
+                sign = -1.0 if m == 0 else 1.0
+                for w, src in enumerate((neg_iv, neg_mu_iv)):
+                    w_t[w] = psum.tile(
+                        [P, PACK, CLASSES], F32, tag=WEIGHT_BANKS[(2 * m + w) % len(WEIGHT_BANKS)], name="wt"
+                    )
+                    for t in range(PACK):
+                        nc.tensor.transpose(w_t[w][:, t, :], src[:, m, t, :], identity[:])
+                for w, factor in enumerate((0.5 * sign, -1.0 * sign)):
+                    nc.scalar.activation(
+                        out=w_grouped[:, w, m, :].rearrange("p (k t) -> p k t", t=PACK),
+                        in_=w_t[w][:].rearrange("p t k -> p k t"),
+                        func=ACT.Copy,
+                        scale=factor,
+                    )
+                nc.scalar.activation(
+                    out=flat(neg_mu2_iv[:, m, :, :]),
+                    in_=flat(neg_mu2_iv[:, m, :, :]),
+                    func=ACT.Copy,
+                    accum_out=neg_quad[:, m : m + 1],
+                )
+
+            quantise_xx(0)
+            for m in range(MODES):
+                for w in range(2):
+                    nc.vector.quantize_mx(
+                        out=w_words[:, w, m, :].bitcast(FP8X4), scales=w_scales[:, w, m, :], in_=w_grouped[:, w, m, :]
+                    )
+                if m >= 1:
+                    mx_group(0, m)
+
+            nc.vector.tensor_tensor(out=neg_quad[:], in0=neg_quad[:], in1=log_det[:], op=ALU.subtract)
+            nc.vector.scalar_tensor_tensor(
+                out=bias[:], in0=neg_quad[:], scalar=0.5, in1=ln_pi[:], op0=ALU.mult, op1=ALU.add
+            )
+            nc.vector.tensor_scalar(out=dbias[:], in0=bias[:], scalar1=bias[:, 0:1], scalar2=None, op0=ALU.subtract)
+
+            copy_and_square_x(1)
+            for h in range(2):
+                transpose_x(2, h)
+            copy_and_square_x(2)
+
+        big = ctx.enter_context(tc.tile_pool(name="big", bufs=LAG + 1))
+
+        for t in range(BLOCKS + LAG):
+            done = t - LAG
+            if is_block(t + AHEAD + 1):
+                load_x(t + AHEAD + 1)
+            if t < GAMMA_LOADS:
+                load_gamma(t)
+            if is_block(t - 1):
+                exponentials(t - 1)
+                sum_modes(t - 1)
+            for n in range(2):
+                if is_block(t):
+                    running_max(t, n + 1)
+                if is_block(done):
+                    finish_tile(done, n)
+            if is_block(t):
+                running_max(t, 3)
+            for n in range(2):
+                if is_block(done):
+                    transpose_expo(done, n + 2)
+                if is_block(t + AHEAD):
+                    transpose_x(t + AHEAD, n)
+            if is_block(done + 1):
+                transpose_rsum(done + 1)
+            for n in range(2):
+                if is_block(t):
+                    subtract_max(t, n + 1)
+                if is_block(done):
+                    finish_tile(done, n + 2)
+            if is_block(t):
+                subtract_max(t, 3)
+            if t == 0:
+                quantise_x(1)
+                quantise_xx(1)
+            for n in range(2):
+                if is_block(t + 1):
+                    mx_group(t + 1, n + 1)
+                if is_block(done + 1):
+                    transpose_expo(done + 1, n)
+            if is_block(t + 1):
+                mx_group(t + 1, 3)
+            if is_block(t + 2):
+                quantise_x(t + 2)
+                quantise_xx(t + 2)
+            if is_block(done + 1):
+                times_gamma(done + 1)
+            if is_block(t + AHEAD):
+                copy_and_square_x(t + AHEAD)
+            first = t - LN_DELAY - (GROUP - 1)
+            if is_block(first) and first % GROUP == 0:
+                reciprocal_sums(first)

@@ -25,14 +25,49 @@ HALF = BLOCK // 2
 GAMMA_LOADS = 4
 FLOPS = 2 * 2 * SAMPLES * CLASSES * MODES * FEATURES
 
-AHEAD = 3
-GROUP = 4
-LN_DELAY = 2
-LAG = (GROUP - 1) + LN_DELAY + 2
+ACC_BANKS = 4
+XT_BANKS = 2
+RO = 1
+MO = 1
+QO = 3
+QSTEP = 2
+AHEAD = 4
+GROUPS = (4,4,4,4)
+GROUP_OF = [g for g, n in enumerate(GROUPS) for i in range(n)]
+FIRST_OF = [sum(GROUPS[:g]) for g in range(len(GROUPS))]
+LAST_OF = [sum(GROUPS[: g + 1]) - 1 for g in range(len(GROUPS))]
+LN_STEP = [last + 2 for last in LAST_OF]
 
-WEIGHT_BANKS = ("et0", "et1", "rt", "p1", "p2", "p3")
-DRAIN_BANKS = ("p1", "p2", "p3", "xt0", "xt1", "et0", "et1")
-FIRST_DRAIN_TILE = TILES_PER_BLOCK * (BLOCKS - LAG) + 2
+WARM = 6
+DUMMY = 0
+WAIT = 1
+TURN_BANKS = ("t0", "t1")
+WEIGHT_BANKS = ("t0", "t1", "p3", "p2")
+DRAIN_BANKS = ("t0", "t1", "p0", "p1", "p2", "p3", "xt0", "xt1")
+
+
+def XV(i, h):
+    return i-AHEAD in LN_STEP
+
+
+def PER_STEP(t):
+    return 5 if t < BLOCKS else 10
+
+
+def RELU_S(t):
+    return t-1 not in LN_STEP
+
+
+def VIA_S(i, jl):
+    return False
+
+
+def SQV(i, h):
+    return h==1 and i<10 and not XV(i,h)
+
+
+def ORDER(t):
+    return "rdWuyuYaebEGuzufcquZL"
 
 
 def tile_dota_mix_pa_t_kernel(tc, x, gamma_class, mu, cur_var, pi, out):
@@ -44,38 +79,40 @@ def tile_dota_mix_pa_t_kernel(tc, x, gamma_class, mu, cur_var, pi, out):
     with ExitStack() as ctx:
         ctx.enter_context(tc.manual_schedule())
         const = ctx.enter_context(tc.tile_pool(name="const", bufs=1))
-        xin = ctx.enter_context(tc.tile_pool(name="xin", bufs=4))
-        grp = ctx.enter_context(tc.tile_pool(name="grp", bufs=3))
-        cod = ctx.enter_context(tc.tile_pool(name="cod", bufs=3))
+        xin = ctx.enter_context(tc.tile_pool(name="xin", bufs=5))
+        grp = ctx.enter_context(tc.tile_pool(name="grp", bufs=4))
+        cod = ctx.enter_context(tc.tile_pool(name="cod", bufs=4))
         two = ctx.enter_context(tc.tile_pool(name="two", bufs=2))
-        tops = ctx.enter_context(tc.tile_pool(name="tops", bufs=4))
-        sums = ctx.enter_context(tc.tile_pool(name="sums", bufs=LAG + 1))
+        tops = ctx.enter_context(tc.tile_pool(name="tops", bufs=5))
         outp = ctx.enter_context(tc.tile_pool(name="outp", bufs=3))
+        stg = ctx.enter_context(tc.tile_pool(name="stg", bufs=2))
         psum = ctx.enter_context(tc.psum_pool(name="psum", bufs=1))
 
         identity = const.tile([P, P], F32, name="identf")
-        w_words = const.tile([P, 2, MODES, CLASSES], U32, name="wq", align_bytes=64)
-        w_scales = const.tile([P, 2, MODES, CLASSES], U8, name="ws", align_bytes=64)
+        idle = const.tile([P, BLOCK], BF16, name="idle")
+        identity_bf = const.tile([P, P], BF16, name="identb")
+        w_words = const.tile([P, MODES, 2, CLASSES], U32, name="wq", align_bytes=64)
+        w_scales = const.tile([P, MODES, 2, CLASSES], U8, name="ws", align_bytes=64)
         dbias = const.tile([P, MODES], F32, name="bd")
         gamma_sb = const.tile([P, TILES, CLASSES], BF16, name="g_sb")
 
         x_sb = {}
         x_t = {}
-        x_grouped = {}
-        xx_grouped = {}
-        operands = {}
+        grouped = {}
+        codes = {}
         group_acc = {}
         top = {}
         expo = {}
         esum = {}
-        rsum_t = {}
         ratio = {}
-        expo_t = {}
         result = {}
 
         def is_block(i):
             return 0 <= i < BLOCKS
 
+        def keep_busy():
+            scrap = psum.tile([P, BLOCK], F32, tag=TURN_BANKS[-1], name="scrap")
+            nc.tensor.matmul(scrap[:], lhsT=idle[:, 0:P], rhs=idle[:], start=True, stop=True)
 
         def load_x(i):
             x_sb[i] = xin.tile([P, TILES_PER_BLOCK, FEATURES], BF16, name="x_sb")
@@ -86,7 +123,7 @@ def tile_dota_mix_pa_t_kernel(tc, x, gamma_class, mu, cur_var, pi, out):
             nc.sync.dma_start(out=gamma_sb[:, js, :], in_=gamma_rows[:, js, :])
 
         def transpose_x(i, h):
-            x_t[(i, h)] = psum.tile([P, 2, HALF], F32, tag="xt%d" % h, name="xt")
+            x_t[(i, h)] = psum.tile([P, 2, HALF], F32, tag="xt%d" % (h % XT_BANKS), name="xt")
             pairs = x_sb[i][:].bitcast(F32)
             for jj in range(2):
                 for u in range(2):
@@ -95,77 +132,73 @@ def tile_dota_mix_pa_t_kernel(tc, x, gamma_class, mu, cur_var, pi, out):
                     )
 
         def copy_x(i, h, on_vector):
-            if h == 0:
-                x_grouped[i] = grp.tile([P, BLOCK, PACK], BF16, name="xg", align_bytes=64)
-                xx_grouped[i] = grp.tile([P, BLOCK, PACK], BF16, name="x2g", align_bytes=64)
+            if i not in grouped:
+                grouped[i] = grp.tile([P, 2, BLOCK, PACK], BF16, name="xg", align_bytes=64)
             cols = slice(h * HALF, (h + 1) * HALF)
-            dst = x_grouped[i][:].bitcast(F32)[:, cols, :]
+            dst = grouped[i][:, 1, cols, :].bitcast(F32)
             src = x_t[(i, h)][:].rearrange("p u c -> p c u")
             if on_vector:
                 nc.vector.tensor_copy(out=dst, in_=src)
             else:
                 nc.scalar.copy(out=dst, in_=src)
 
-        def square_x(i, h):
+        def square_x(i, h, on_vector):
             cols = slice(h * HALF, (h + 1) * HALF)
-            nc.scalar.activation(
-                out=xx_grouped[i][:, cols, :].rearrange("p c (u e) -> p c u e", e=2),
-                in_=x_t[(i, h)][:].bitcast(BF16).rearrange("p u (c e) -> p c u e", e=2),
-                func=ACT.Square,
-            )
+            dst = grouped[i][:, 0, cols, :].rearrange("p c (u e) -> p c u e", e=2)
+            src = x_t[(i, h)][:].bitcast(BF16).rearrange("p u (c e) -> p c u e", e=2)
+            if on_vector:
+                x_g = grouped[i][:, 1, cols, :].rearrange("p c (u e) -> p c u e", e=2)
+                nc.vector.tensor_tensor(out=dst, in0=src, in1=x_g, op=ALU.mult)
+            else:
+                nc.scalar.activation(out=dst, in_=src, func=ACT.Square)
 
-        def copy_and_square_x(i):
-            for h in range(2):
-                copy_x(i, h, False)
-                square_x(i, h)
+        def copy_and_square(i, h, on_vector):
+            copy_x(i, h, on_vector)
+            square_x(i, h, on_vector)
 
-        def quantise_x(i):
-            x_words = cod.tile([P, BLOCK], U32, name="xq", align_bytes=64)
-            x_scales = cod.tile([P, BLOCK], U8, name="xs", align_bytes=64)
-            xx_words = cod.tile([P, BLOCK], U32, name="x2q", align_bytes=64)
-            xx_scales = cod.tile([P, BLOCK], U8, name="x2s", align_bytes=64)
-            operands[i] = ((xx_words, xx_scales), (x_words, x_scales))
+        def quantise(i):
+            words = cod.tile([P, 2, BLOCK], U32, name="xq", align_bytes=64)
+            scales = cod.tile([P, 2, BLOCK], U8, name="xs", align_bytes=64)
+            codes[i] = (words, scales)
             nc.vector.quantize_mx(
-                out=x_words[:].bitcast(FP8X4), scales=x_scales[:], in_=x_grouped[i][:].rearrange("p c t -> p (c t)")
+                out=words[:].rearrange("p w c -> p (w c)").bitcast(FP8X4),
+                scales=scales[:].rearrange("p w c -> p (w c)"),
+                in_=grouped[i][:].rearrange("p w c t -> p (w c t)"),
             )
-
-        def quantise_xx(i):
-            xx_words, xx_scales = operands[i][0]
-            nc.vector.quantize_mx(
-                out=xx_words[:].bitcast(FP8X4), scales=xx_scales[:], in_=xx_grouped[i][:].rearrange("p c t -> p (c t)")
-            )
-
 
         def mx_group(i, m):
-            group_acc[(i, m)] = psum.tile([P, BLOCK], F32, tag="p%d" % m, name="acc")
+            group_acc[(i, m)] = psum.tile([P, BLOCK], F32, tag="p%d" % ((3 * i + m - 1) % ACC_BANKS), name="acc")
+            words, scales = codes[i]
             passes = ((0, m), (0, 0), (1, m), (1, 0))
             for n, (w, mode) in enumerate(passes):
-                words, scales = operands[i][w]
                 nc.tensor.matmul_mx(
                     out=group_acc[(i, m)][:],
-                    lhsT=w_words[:, w, mode, :].bitcast(FP8X4),
-                    lhsT_scale=w_scales[:, w, mode, :],
-                    rhs=words[:].bitcast(FP8X4),
-                    rhs_scale=scales[:],
+                    lhsT=w_words[:, mode, w, :].bitcast(FP8X4),
+                    lhsT_scale=w_scales[:, mode, w, :],
+                    rhs=words[:, w, :].bitcast(FP8X4),
+                    rhs_scale=scales[:, w, :],
                     start=(n == 0),
                     stop=(n == len(passes) - 1),
                 )
 
-        def running_max(i, m):
-            if m == 1:
-                top[i] = tops.tile([P, BLOCK], F32, name="top")
+        def first_max(i, on_vector):
+            top[i] = tops.tile([P, BLOCK], F32, name="top")
+            if on_vector:
                 nc.vector.tensor_scalar(
                     out=top[i][:], in0=group_acc[(i, 1)][:], scalar1=dbias[:, 1:2], scalar2=0.0, op0=ALU.add, op1=ALU.max
                 )
-            else:
-                nc.vector.scalar_tensor_tensor(
-                    out=top[i][:],
-                    in0=group_acc[(i, m)][:],
-                    scalar=dbias[:, m : m + 1],
-                    in1=top[i][:],
-                    op0=ALU.add,
-                    op1=ALU.max,
-                )
+                return
+            nc.scalar.activation(out=top[i][:], in_=group_acc[(i, 1)][:], func=ACT.Relu, bias=dbias[:, 1:2])
+
+        def running_max(i, m):
+            nc.vector.scalar_tensor_tensor(
+                out=top[i][:],
+                in0=group_acc[(i, m)][:],
+                scalar=dbias[:, m : m + 1],
+                in1=top[i][:],
+                op0=ALU.add,
+                op1=ALU.max,
+            )
 
         def subtract_max(i, m):
             if m == 1:
@@ -186,42 +219,87 @@ def tile_dota_mix_pa_t_kernel(tc, x, gamma_class, mu, cur_var, pi, out):
         def sum_modes(i):
             half_sums = two.tile([P, 2, BLOCK], F32, name="hs")
             nc.gpsimd.tensor_tensor(out=half_sums[:], in0=expo[i][:, 0:2, :], in1=expo[i][:, 2:4, :], op=ALU.add)
-            esum[i] = sums.tile([P, BLOCK], F32, name="ssum")
-            nc.gpsimd.tensor_tensor(out=esum[i][:], in0=half_sums[:, 0, :], in1=half_sums[:, 1, :], op=ALU.add)
-
-        def reciprocal_sums(first):
-            for i in range(first, first + GROUP):
-                nc.scalar.activation(out=esum[i][:], in_=esum[i][:], func=ACT.Ln)
-            for i in range(first, first + GROUP):
-                nc.scalar.activation(out=esum[i][:], in_=esum[i][:], func=ACT.Exp, scale=-1.0)
-
-
-        def transpose_rsum(i):
-            rsum_t[i] = psum.tile([P, TILES_PER_BLOCK, CLASSES], F32, tag="rt", name="rt")
-            for jl in range(TILES_PER_BLOCK):
-                nc.tensor.transpose(rsum_t[i][:, jl, :], esum[i][:, jl * P : (jl + 1) * P], identity[:])
-
-        def times_gamma(i):
-            ratio[i] = two.tile([P, TILES_PER_BLOCK, CLASSES], F32, name="rr")
-            js = slice(i * TILES_PER_BLOCK, (i + 1) * TILES_PER_BLOCK)
-            nc.vector.tensor_tensor(out=ratio[i][:], in0=rsum_t[i][:], in1=gamma_sb[:, js, :], op=ALU.mult)
-            result[i] = outp.tile([P, TILES_PER_BLOCK, CLASSES * MODES], F32, name="o_sb")
-
-        def transpose_expo(i, jl):
-            drained = TILES_PER_BLOCK * i + jl - FIRST_DRAIN_TILE
-            bank = DRAIN_BANKS[drained % len(DRAIN_BANKS)] if drained >= 0 else "et%d" % (jl % 2)
-            expo_t[(i, jl)] = psum.tile([P, MODES, CLASSES], F32, tag=bank, name="et")
-            for m in range(MODES):
-                nc.tensor.transpose(expo_t[(i, jl)][:, m, :], expo[i][:, m, jl * P : (jl + 1) * P], identity[:])
-
-        def finish_tile(i, jl):
-            nc.vector.tensor_tensor(
-                out=result[i][:, jl, :].rearrange("p (k m) -> p k m", m=MODES),
-                in0=expo_t[(i, jl)][:].rearrange("p m k -> p k m"),
-                in1=ratio[i][:, jl, :].unsqueeze(2).to_broadcast([P, CLASSES, MODES]),
-                op=ALU.mult,
+            g = GROUP_OF[i]
+            if i == FIRST_OF[g]:
+                esum[g] = sums.tile([P, max(GROUPS), BLOCK], F32, name="ssum")
+            nc.gpsimd.tensor_tensor(
+                out=esum[g][:, i - FIRST_OF[g], :], in0=half_sums[:, 0, :], in1=half_sums[:, 1, :], op=ALU.add
             )
-            nc.sync.dma_start(out=out_rows[:, i * TILES_PER_BLOCK + jl, :], in_=result[i][:, jl, :])
+
+        def ln_sums(g):
+            used = esum[g][:, 0 : GROUPS[g], :]
+            nc.scalar.activation(out=used, in_=used, func=ACT.Ln)
+
+        def reciprocal_sum(i):
+            s = esum[GROUP_OF[i]][:, i - FIRST_OF[GROUP_OF[i]], :]
+            nc.scalar.activation(out=s, in_=s, func=ACT.Exp, scale=-1.0)
+
+        units = []
+        for i in range(BLOCKS):
+            if i == 0:
+                units.append(("r", 0))
+            for jl in range(TILES_PER_BLOCK):
+                if jl == 2 and i + 1 < BLOCKS:
+                    units.append(("r", i + 1))
+                units.append(("e", i, jl))
+        turned = {}
+        state = {"avail": 0, "turn": 0, "done": 0, "bank": 0, "recip": 0}
+
+        def unit_block(n):
+            return units[n][1]
+
+        def turn(n, banks):
+            bank = banks[state["bank"] % len(banks)]
+            state["bank"] += 1
+            u = units[n]
+            turned[n] = psum.tile([P, MODES, CLASSES], F32, tag=bank, name="tb")
+            for q in range(4):
+                if u[0] == "r":
+                    i = u[1]
+                    src = esum[GROUP_OF[i]][:, i - FIRST_OF[GROUP_OF[i]], q * P : (q + 1) * P]
+                else:
+                    src = expo[u[1]][:, q, u[2] * P : (u[2] + 1) * P]
+                nc.tensor.transpose(turned[n][:, q, :], src, identity[:])
+
+        def finish(n):
+            u = units[n]
+            i = u[1]
+            if u[0] == "r":
+                ratio[i] = two.tile([P, TILES_PER_BLOCK, CLASSES], F32, name="rr")
+                js = slice(i * TILES_PER_BLOCK, (i + 1) * TILES_PER_BLOCK)
+                nc.vector.tensor_tensor(out=ratio[i][:], in0=turned[n][:], in1=gamma_sb[:, js, :], op=ALU.mult)
+                result[i] = outp.tile([P, TILES_PER_BLOCK, CLASSES * MODES], F32, name="o_sb")
+            elif VIA_S(i, u[2]):
+                jl = u[2]
+                stage = stg.tile([P, CLASSES, MODES], F32, name="stage")
+                nc.scalar.copy(out=stage[:], in_=turned[n][:].rearrange("p m k -> p k m"))
+                nc.gpsimd.tensor_tensor(
+                    out=result[i][:, jl, :].rearrange("p (k m) -> p k m", m=MODES),
+                    in0=stage[:],
+                    in1=ratio[i][:, jl, :].unsqueeze(2).to_broadcast([P, CLASSES, MODES]),
+                    op=ALU.mult,
+                )
+                nc.sync.dma_start(out=out_rows[:, i * TILES_PER_BLOCK + jl, :], in_=result[i][:, jl, :])
+            else:
+                jl = u[2]
+                nc.vector.tensor_tensor(
+                    out=result[i][:, jl, :].rearrange("p (k m) -> p k m", m=MODES),
+                    in0=turned[n][:].rearrange("p m k -> p k m"),
+                    in1=ratio[i][:, jl, :].unsqueeze(2).to_broadcast([P, CLASSES, MODES]),
+                    op=ALU.mult,
+                )
+                nc.sync.dma_start(out=out_rows[:, i * TILES_PER_BLOCK + jl, :], in_=result[i][:, jl, :])
+
+        def pump(banks):
+            while state["turn"] < state["avail"] and state["turn"] < state["done"] + len(banks):
+                turn(state["turn"], banks)
+                state["turn"] += 1
+
+        def next_unit(banks):
+            if state["done"] < state["turn"]:
+                finish(state["done"])
+                state["done"] += 1
+                pump(banks)
 
         with tc.tile_pool(name="prep", bufs=1) as prep:
             var_sb = prep.tile([P, MODES, FEATURES], BF16, name="var_sb")
@@ -234,29 +312,20 @@ def tile_dota_mix_pa_t_kernel(tc, x, gamma_class, mu, cur_var, pi, out):
             nc.sync.dma_start(out=mu_sb[:], in_=mu)
             for i in range(1, AHEAD + 1):
                 load_x(i)
+            nc.vector.memset(idle[:], 0.0)
             make_identity(nc, identity[:])
+            nc.gpsimd.tensor_copy(out=identity_bf[:], in_=identity[:])
 
             ln_var = prep.tile([P, MODES, FEATURES], F32, name="lnv")
-            seed = prep.tile([P, MODES, PACK, P], F32, name="y0p")
-            neg_iv = prep.tile([P, MODES, PACK, P], F32, name="nivp")
-            neg_mu_iv = prep.tile([P, MODES, PACK, P], F32, name="nmivp")
-            neg_mu2_iv = prep.tile([P, MODES, PACK, P], F32, name="tmp")
-            w_grouped = prep.tile([P, 2, MODES, CLASSES * PACK], BF16, name="wg", align_bytes=64)
+            inv_var = prep.tile([P, MODES, FEATURES], F32, name="ivp")
+            mu_iv = prep.tile([P, MODES, FEATURES], F32, name="miv")
+            w_rows = prep.tile([P, MODES, 2, FEATURES], BF16, name="wr", align_bytes=64)
+            w_grouped = prep.tile([P, MODES, 2, CLASSES * PACK], BF16, name="wg", align_bytes=64)
             log_det = prep.tile([P, MODES], F32, name="ld")
             pi_eps = prep.tile([P, MODES], F32, name="pif")
             ln_pi = prep.tile([P, MODES], F32, name="lnpi")
-            neg_quad = prep.tile([P, MODES], F32, name="qs")
+            quad = prep.tile([P, MODES], F32, name="qs")
             bias = prep.tile([P, MODES], F32, name="bias")
-            w_t = {}
-
-            def by_value(ap):
-                return ap.rearrange("k (q t) -> k t q", t=PACK)
-
-            def split(ap):
-                return ap
-
-            def flat(ap):
-                return ap.rearrange("k t q -> k (t q)")
 
             nc.gpsimd.tensor_scalar(out=pi_eps[:], in0=pi_sb[:], scalar1=1e-10, scalar2=0.0, op0=ALU.add, op1=ALU.add)
             for m in range(MODES):
@@ -264,131 +333,167 @@ def tile_dota_mix_pa_t_kernel(tc, x, gamma_class, mu, cur_var, pi, out):
                     out=ln_var[:, m, :], in_=var_sb[:, m, :], func=ACT.Ln, accum_out=log_det[:, m : m + 1]
                 )
             nc.scalar.activation(out=ln_pi[:], in_=pi_eps[:], func=ACT.Ln)
+            for m in range(MODES):
+                nc.scalar.activation(out=inv_var[:, m, :], in_=ln_var[:, m, :], func=ACT.Exp, scale=-1.0)
 
             for h in range(2):
                 transpose_x(0, h)
-            for h in range(2):
                 copy_x(0, h, True)
-            quantise_x(0)
-
-            for m in range(MODES):
-                nc.scalar.activation(out=split(seed[:, m, :, :]), in_=by_value(ln_var[:, m, :]), func=ACT.Exp, scale=-1.0)
+            transpose_x(1, 0)
             for h in range(2):
-                square_x(0, h)
-            for h in range(2):
-                transpose_x(1, h)
+                square_x(0, h, True)
+            transpose_x(1, 1)
+            copy_and_square(1, 0, False)
 
-            for m in range(MODES):
-                nc.vector.tensor_tensor(
-                    out=split(neg_iv[:, m, :, :]), in0=by_value(var_sb[:, m, :]), in1=split(seed[:, m, :, :]), op=ALU.mult
+            def weight_rows(m):
+                sign = -1.0 if m == 0 else 1.0
+                nc.vector.tensor_scalar(
+                    out=w_rows[:, m, 0, :], in0=inv_var[:, m, :], scalar1=-0.5 * sign, scalar2=None, op0=ALU.mult
                 )
                 nc.vector.scalar_tensor_tensor(
-                    out=flat(neg_iv[:, m, :, :]),
-                    in0=flat(neg_iv[:, m, :, :]),
-                    scalar=2.0,
-                    in1=flat(seed[:, m, :, :]),
-                    op0=ALU.subtract,
-                    op1=ALU.mult,
-                )
-                nc.vector.tensor_tensor(
-                    out=split(neg_mu_iv[:, m, :, :]), in0=by_value(mu_sb[:, m, :]), in1=split(neg_iv[:, m, :, :]), op=ALU.mult
-                )
-                nc.gpsimd.tensor_tensor(
-                    out=split(neg_mu2_iv[:, m, :, :]),
-                    in0=by_value(mu_sb[:, m, :]),
-                    in1=split(neg_mu_iv[:, m, :, :]),
-                    op=ALU.mult,
-                )
-                sign = -1.0 if m == 0 else 1.0
-                for w, src in enumerate((neg_iv, neg_mu_iv)):
-                    w_t[w] = psum.tile(
-                        [P, PACK, CLASSES], F32, tag=WEIGHT_BANKS[(2 * m + w) % len(WEIGHT_BANKS)], name="wt"
-                    )
-                    for t in range(PACK):
-                        nc.tensor.transpose(w_t[w][:, t, :], src[:, m, t, :], identity[:])
-                for w, factor in enumerate((0.5 * sign, -1.0 * sign)):
-                    nc.scalar.activation(
-                        out=w_grouped[:, w, m, :].rearrange("p (k t) -> p k t", t=PACK),
-                        in_=w_t[w][:].rearrange("p t k -> p k t"),
-                        func=ACT.Copy,
-                        scale=factor,
-                    )
-                nc.scalar.activation(
-                    out=flat(neg_mu2_iv[:, m, :, :]),
-                    in_=flat(neg_mu2_iv[:, m, :, :]),
-                    func=ACT.Copy,
-                    accum_out=neg_quad[:, m : m + 1],
+                    out=mu_iv[:, m, :], in0=mu_sb[:, m, :], scalar=sign, in1=inv_var[:, m, :], op0=ALU.mult, op1=ALU.mult
                 )
 
-            quantise_xx(0)
-            for m in range(MODES):
+            def weight_rows_mu(m):
+                nc.vector.tensor_copy(out=w_rows[:, m, 1, :], in_=mu_iv[:, m, :])
+
+            def turn_weights(m):
+                w_t = psum.tile([P, 2, PACK, CLASSES], BF16, tag=WEIGHT_BANKS[m], name="wt")
                 for w in range(2):
-                    nc.vector.quantize_mx(
-                        out=w_words[:, w, m, :].bitcast(FP8X4), scales=w_scales[:, w, m, :], in_=w_grouped[:, w, m, :]
-                    )
+                    for t in range(PACK):
+                        nc.tensor.transpose(w_t[:, w, t, :], w_rows[:, m, w, t::PACK], identity_bf[:])
+                nc.scalar.copy(
+                    out=w_grouped[:, m, :, :].rearrange("p w (k t) -> p w k t", t=PACK),
+                    in_=w_t[:].rearrange("p w t k -> p w k t"),
+                )
+
+            weight_rows(0)
+            weight_rows(1)
+            weight_rows_mu(0)
+            turn_weights(0)
+            weight_rows(2)
+            weight_rows_mu(1)
+            turn_weights(1)
+            transpose_x(2, 0)
+            weight_rows(3)
+            weight_rows_mu(2)
+            turn_weights(2)
+            quantise(0)
+            weight_rows_mu(3)
+            turn_weights(3)
+            copy_and_square(1, 1, True)
+            for n in range(WARM):
+                keep_busy()
+            for m in range(MODES):
+                nc.vector.quantize_mx(
+                    out=w_words[:, m, :, :].rearrange("p w k -> p (w k)").bitcast(FP8X4),
+                    scales=w_scales[:, m, :, :].rearrange("p w k -> p (w k)"),
+                    in_=w_grouped[:, m, :, :].rearrange("p w k -> p (w k)"),
+                )
                 if m >= 1:
                     mx_group(0, m)
-
-            nc.vector.tensor_tensor(out=neg_quad[:], in0=neg_quad[:], in1=log_det[:], op=ALU.subtract)
+                nc.vector.scalar_tensor_tensor(
+                    out=inv_var[:, m, :],
+                    in0=mu_sb[:, m, :],
+                    scalar=-1.0 if m == 0 else 1.0,
+                    in1=mu_iv[:, m, :],
+                    op0=ALU.mult,
+                    op1=ALU.mult,
+                    accum_out=quad[:, m : m + 1],
+                )
+                if m == 1:
+                    transpose_x(2, 1)
+            nc.vector.tensor_tensor(out=quad[:], in0=quad[:], in1=log_det[:], op=ALU.add)
             nc.vector.scalar_tensor_tensor(
-                out=bias[:], in0=neg_quad[:], scalar=0.5, in1=ln_pi[:], op0=ALU.mult, op1=ALU.add
+                out=bias[:], in0=quad[:], scalar=-0.5, in1=ln_pi[:], op0=ALU.mult, op1=ALU.add
             )
             nc.vector.tensor_scalar(out=dbias[:], in0=bias[:], scalar1=bias[:, 0:1], scalar2=None, op0=ALU.subtract)
-
-            copy_and_square_x(1)
+            quantise(1)
+            copy_and_square(2, 0, False)
+            if RELU_S(0) and RO == 1:
+                first_max(0, False)
+            for n in range(3, ACC_BANKS):
+                mx_group(n // 3, n % 3 + 1)
+            transpose_x(3, 0)
+            copy_and_square(2, 1, False)
+            transpose_x(3, 1)
+            if MO == 1:
+                if not RELU_S(0):
+                    first_max(0, True)
+                running_max(0, 2)
+                running_max(0, 3)
             for h in range(2):
-                transpose_x(2, h)
-            copy_and_square_x(2)
+                copy_and_square(3, h, False)
+            for i in range(2, QO):
+                quantise(i)
 
-        big = ctx.enter_context(tc.tile_pool(name="big", bufs=LAG + 1))
+        big = ctx.enter_context(tc.tile_pool(name="big", bufs=9))
+        sums = ctx.enter_context(tc.tile_pool(name="sums", bufs=2))
 
-        for t in range(BLOCKS + LAG):
-            done = t - LAG
+        limit = 0
+        t = -1
+        while state["done"] < len(units):
+            t += 1
+            banks = TURN_BANKS if t < BLOCKS else DRAIN_BANKS
+            ln_group = LN_STEP.index(t) if t in LN_STEP else None
             if is_block(t + AHEAD + 1):
                 load_x(t + AHEAD + 1)
             if t < GAMMA_LOADS:
                 load_gamma(t)
-            if is_block(t - 1):
-                exponentials(t - 1)
-                sum_modes(t - 1)
-            for n in range(2):
-                if is_block(t):
-                    running_max(t, n + 1)
-                if is_block(done):
-                    finish_tile(done, n)
-            if is_block(t):
-                running_max(t, 3)
-            for n in range(2):
-                if is_block(done):
-                    transpose_expo(done, n + 2)
-                if is_block(t + AHEAD):
-                    transpose_x(t + AHEAD, n)
-            if is_block(done + 1):
-                transpose_rsum(done + 1)
-            for n in range(2):
-                if is_block(t):
-                    subtract_max(t, n + 1)
-                if is_block(done):
-                    finish_tile(done, n + 2)
-            if is_block(t):
-                subtract_max(t, 3)
-            if t == 0:
-                quantise_x(1)
-                quantise_xx(1)
-            for n in range(2):
-                if is_block(t + 1):
-                    mx_group(t + 1, n + 1)
-                if is_block(done + 1):
-                    transpose_expo(done + 1, n)
-            if is_block(t + 1):
-                mx_group(t + 1, 3)
-            if is_block(t + 2):
-                quantise_x(t + 2)
-                quantise_xx(t + 2)
-            if is_block(done + 1):
-                times_gamma(done + 1)
-            if is_block(t + AHEAD):
-                copy_and_square_x(t + AHEAD)
-            first = t - LN_DELAY - (GROUP - 1)
-            if is_block(first) and first % GROUP == 0:
-                reciprocal_sums(first)
+            count = PER_STEP(t)
+            left = count
+            order = ORDER(t)
+            pump(banks)
+            for pos, k in enumerate(order):
+                if k == "a" and is_block(t + MO) and not RELU_S(t + MO):
+                    first_max(t + MO, True)
+                elif k == "r" and is_block(t + RO) and RELU_S(t + RO):
+                    first_max(t + RO, False)
+                elif k in "bc" and is_block(t + MO):
+                    running_max(t + MO, 2 + "bc".index(k))
+                elif k in "def":
+                    q = "def".index(k)
+                    if is_block(t):
+                        subtract_max(t, q + 1)
+                    n = 3 * t + q + ACC_BANKS
+                    if is_block(n // 3) and t >= 0:
+                        mx_group(n // 3, n % 3 + 1)
+                elif k == "q" and is_block(t + QO):
+                    quantise(t + QO)
+                elif k == "u":
+                    if t >= BLOCKS and DUMMY and left % DUMMY == 0:
+                        keep_busy()
+                    if left > 0:
+                        left -= 1
+                        next_unit(banks)
+                elif k in "yz" and is_block(t + AHEAD):
+                    transpose_x(t + AHEAD, "yz".index(k))
+                elif k in "YZ" and is_block(t + AHEAD):
+                    h = "YZ".index(k)
+                    if SQV(t + AHEAD, h):
+                        copy_x(t + AHEAD, h, False)
+                    else:
+                        copy_and_square(t + AHEAD, h, XV(t + AHEAD, h))
+                elif k in "VW" and is_block(t + AHEAD - 1) and t >= 1:
+                    h = "VW".index(k)
+                    if SQV(t + AHEAD - 1, h):
+                        square_x(t + AHEAD - 1, h, True)
+                elif k == "E" and is_block(t - 1):
+                    exponentials(t - 1)
+                elif k == "G" and is_block(t - 1):
+                    sum_modes(t - 1)
+                elif k == "L":
+                    if ln_group is not None:
+                        ln_sums(ln_group)
+                        limit = LAST_OF[ln_group] + 1
+                    while state["recip"] < limit and units.index(("r", state["recip"])) < state["done"] + 2 * count + 3:
+                        reciprocal_sum(state["recip"])
+                        state["recip"] += 1
+            for n in range(left):
+                if t >= BLOCKS and DUMMY and (left - n) % DUMMY == 0:
+                    keep_busy()
+                next_unit(banks)
+            if t >= BLOCKS or t - 1 in LN_STEP or WAIT == 0:
+                state["avail"] = len(units) if limit == BLOCKS else units.index(("r", limit))
+            if t >= BLOCKS:
+                pump(banks)

@@ -27,47 +27,54 @@ FLOPS = 2 * 2 * SAMPLES * CLASSES * MODES * FEATURES
 
 ACC_BANKS = 4
 XT_BANKS = 2
-RO = 1
-MO = 1
-QO = 3
+LOOK = 2
 QSTEP = 2
-AHEAD = 4
-GROUPS = (4,4,4,4)
+READY = 5
+AHEAD = 5
+GROUPS = (4,4,4,3,1)
 GROUP_OF = [g for g, n in enumerate(GROUPS) for i in range(n)]
 FIRST_OF = [sum(GROUPS[:g]) for g in range(len(GROUPS))]
 LAST_OF = [sum(GROUPS[: g + 1]) - 1 for g in range(len(GROUPS))]
 LN_STEP = [last + 2 for last in LAST_OF]
 
-WARM = 6
+SCRAP = ["t1"]
+WARM = 4
+PRE = True
+WARM2 = 0
+X1V = False
+X2V = True
+X3V = True
+X4V = False
+RAT = 7
 DUMMY = 0
 WAIT = 1
 TURN_BANKS = ("t0", "t1")
 WEIGHT_BANKS = ("t0", "t1", "p3", "p2")
-DRAIN_BANKS = ("t0", "t1", "p0", "p1", "p2", "p3", "xt0", "xt1")
+DRAIN_BANKS = ("t0", "t1", "p0", "p1", "p2", "p3")
 
 
 def XV(i, h):
-    return i-AHEAD in LN_STEP
+    return False
+
+
+def SQV(i, h):
+    return h == 1
 
 
 def PER_STEP(t):
-    return 5 if t < BLOCKS else 10
+    return 4 if t < BLOCKS else 8
 
 
 def RELU_S(t):
-    return t-1 not in LN_STEP
+    return t - 1 not in LN_STEP
 
 
 def VIA_S(i, jl):
     return False
 
 
-def SQV(i, h):
-    return h==1 and i<10 and not XV(i,h)
-
-
 def ORDER(t):
-    return "rdWuyuYaebEGuzufcquZL"
+    return "rdWauebEGLuqfcuxP" if t in LN_STEP else "rdWuYauebEGuzxuqfcuZP"
 
 
 def tile_dota_mix_pa_t_kernel(tc, x, gamma_class, mu, cur_var, pi, out):
@@ -79,11 +86,12 @@ def tile_dota_mix_pa_t_kernel(tc, x, gamma_class, mu, cur_var, pi, out):
     with ExitStack() as ctx:
         ctx.enter_context(tc.manual_schedule())
         const = ctx.enter_context(tc.tile_pool(name="const", bufs=1))
-        xin = ctx.enter_context(tc.tile_pool(name="xin", bufs=5))
-        grp = ctx.enter_context(tc.tile_pool(name="grp", bufs=4))
-        cod = ctx.enter_context(tc.tile_pool(name="cod", bufs=4))
+        xin = ctx.enter_context(tc.tile_pool(name="xin", bufs=4))
+        grp = ctx.enter_context(tc.tile_pool(name="grp", bufs=3))
+        cod = ctx.enter_context(tc.tile_pool(name="cod", bufs=5))
         two = ctx.enter_context(tc.tile_pool(name="two", bufs=2))
         tops = ctx.enter_context(tc.tile_pool(name="tops", bufs=5))
+        rat = ctx.enter_context(tc.tile_pool(name="rat", bufs=RAT))
         outp = ctx.enter_context(tc.tile_pool(name="outp", bufs=3))
         stg = ctx.enter_context(tc.tile_pool(name="stg", bufs=2))
         psum = ctx.enter_context(tc.psum_pool(name="psum", bufs=1))
@@ -111,7 +119,7 @@ def tile_dota_mix_pa_t_kernel(tc, x, gamma_class, mu, cur_var, pi, out):
             return 0 <= i < BLOCKS
 
         def keep_busy():
-            scrap = psum.tile([P, BLOCK], F32, tag=TURN_BANKS[-1], name="scrap")
+            scrap = psum.tile([P, BLOCK], F32, tag=SCRAP[0], name="scrap")
             nc.tensor.matmul(scrap[:], lhsT=idle[:, 0:P], rhs=idle[:], start=True, stop=True)
 
         def load_x(i):
@@ -226,69 +234,45 @@ def tile_dota_mix_pa_t_kernel(tc, x, gamma_class, mu, cur_var, pi, out):
                 out=esum[g][:, i - FIRST_OF[g], :], in0=half_sums[:, 0, :], in1=half_sums[:, 1, :], op=ALU.add
             )
 
-        def ln_sums(g):
-            used = esum[g][:, 0 : GROUPS[g], :]
-            nc.scalar.activation(out=used, in_=used, func=ACT.Ln)
+        def ln_sum(i, bank):
+            s_t = psum.tile([P, TILES_PER_BLOCK, CLASSES], F32, tag=bank, name="st")
+            g = GROUP_OF[i]
+            for jl in range(TILES_PER_BLOCK):
+                nc.tensor.transpose(s_t[:, jl, :], esum[g][:, i - FIRST_OF[g], jl * P : (jl + 1) * P], identity[:])
+            ratio[i] = rat.tile([P, TILES_PER_BLOCK, CLASSES], F32, name="rr")
+            nc.scalar.activation(out=ratio[i][:], in_=s_t[:], func=ACT.Ln)
 
         def reciprocal_sum(i):
-            s = esum[GROUP_OF[i]][:, i - FIRST_OF[GROUP_OF[i]], :]
-            nc.scalar.activation(out=s, in_=s, func=ACT.Exp, scale=-1.0)
+            nc.scalar.activation(out=ratio[i][:], in_=ratio[i][:], func=ACT.Exp, scale=-1.0)
+            js = slice(i * TILES_PER_BLOCK, (i + 1) * TILES_PER_BLOCK)
+            nc.gpsimd.tensor_tensor(out=ratio[i][:], in0=ratio[i][:], in1=gamma_sb[:, js, :], op=ALU.mult)
 
-        units = []
-        for i in range(BLOCKS):
-            if i == 0:
-                units.append(("r", 0))
-            for jl in range(TILES_PER_BLOCK):
-                if jl == 2 and i + 1 < BLOCKS:
-                    units.append(("r", i + 1))
-                units.append(("e", i, jl))
+        units = [(i, jl) for i in range(BLOCKS) for jl in range(TILES_PER_BLOCK)]
         turned = {}
         state = {"avail": 0, "turn": 0, "done": 0, "bank": 0, "recip": 0}
-
-        def unit_block(n):
-            return units[n][1]
 
         def turn(n, banks):
             bank = banks[state["bank"] % len(banks)]
             state["bank"] += 1
-            u = units[n]
+            i, jl = units[n]
             turned[n] = psum.tile([P, MODES, CLASSES], F32, tag=bank, name="tb")
-            for q in range(4):
-                if u[0] == "r":
-                    i = u[1]
-                    src = esum[GROUP_OF[i]][:, i - FIRST_OF[GROUP_OF[i]], q * P : (q + 1) * P]
-                else:
-                    src = expo[u[1]][:, q, u[2] * P : (u[2] + 1) * P]
-                nc.tensor.transpose(turned[n][:, q, :], src, identity[:])
+            for q in range(MODES):
+                nc.tensor.transpose(turned[n][:, q, :], expo[i][:, q, jl * P : (jl + 1) * P], identity[:])
 
         def finish(n):
-            u = units[n]
-            i = u[1]
-            if u[0] == "r":
-                ratio[i] = two.tile([P, TILES_PER_BLOCK, CLASSES], F32, name="rr")
-                js = slice(i * TILES_PER_BLOCK, (i + 1) * TILES_PER_BLOCK)
-                nc.vector.tensor_tensor(out=ratio[i][:], in0=turned[n][:], in1=gamma_sb[:, js, :], op=ALU.mult)
+            i, jl = units[n]
+            if jl == 0:
                 result[i] = outp.tile([P, TILES_PER_BLOCK, CLASSES * MODES], F32, name="o_sb")
-            elif VIA_S(i, u[2]):
-                jl = u[2]
+            dst = result[i][:, jl, :].rearrange("p (k m) -> p k m", m=MODES)
+            src = turned[n][:].rearrange("p m k -> p k m")
+            factor = ratio[i][:, jl, :].unsqueeze(2).to_broadcast([P, CLASSES, MODES])
+            if VIA_S(i, jl):
                 stage = stg.tile([P, CLASSES, MODES], F32, name="stage")
-                nc.scalar.copy(out=stage[:], in_=turned[n][:].rearrange("p m k -> p k m"))
-                nc.gpsimd.tensor_tensor(
-                    out=result[i][:, jl, :].rearrange("p (k m) -> p k m", m=MODES),
-                    in0=stage[:],
-                    in1=ratio[i][:, jl, :].unsqueeze(2).to_broadcast([P, CLASSES, MODES]),
-                    op=ALU.mult,
-                )
-                nc.sync.dma_start(out=out_rows[:, i * TILES_PER_BLOCK + jl, :], in_=result[i][:, jl, :])
+                nc.scalar.copy(out=stage[:], in_=src)
+                nc.gpsimd.tensor_tensor(out=dst, in0=stage[:], in1=factor, op=ALU.mult)
             else:
-                jl = u[2]
-                nc.vector.tensor_tensor(
-                    out=result[i][:, jl, :].rearrange("p (k m) -> p k m", m=MODES),
-                    in0=turned[n][:].rearrange("p m k -> p k m"),
-                    in1=ratio[i][:, jl, :].unsqueeze(2).to_broadcast([P, CLASSES, MODES]),
-                    op=ALU.mult,
-                )
-                nc.sync.dma_start(out=out_rows[:, i * TILES_PER_BLOCK + jl, :], in_=result[i][:, jl, :])
+                nc.vector.tensor_tensor(out=dst, in0=src, in1=factor, op=ALU.mult)
+            nc.sync.dma_start(out=out_rows[:, i * TILES_PER_BLOCK + jl, :], in_=result[i][:, jl, :])
 
         def pump(banks):
             while state["turn"] < state["avail"] and state["turn"] < state["done"] + len(banks):
@@ -310,7 +294,7 @@ def tile_dota_mix_pa_t_kernel(tc, x, gamma_class, mu, cur_var, pi, out):
                 nc.sync.dma_start(out=var_sb[:, m, :], in_=cur_var[:, m, :])
             load_x(0)
             nc.sync.dma_start(out=mu_sb[:], in_=mu)
-            for i in range(1, AHEAD + 1):
+            for i in range(1, 4):
                 load_x(i)
             nc.vector.memset(idle[:], 0.0)
             make_identity(nc, identity[:])
@@ -336,15 +320,6 @@ def tile_dota_mix_pa_t_kernel(tc, x, gamma_class, mu, cur_var, pi, out):
             for m in range(MODES):
                 nc.scalar.activation(out=inv_var[:, m, :], in_=ln_var[:, m, :], func=ACT.Exp, scale=-1.0)
 
-            for h in range(2):
-                transpose_x(0, h)
-                copy_x(0, h, True)
-            transpose_x(1, 0)
-            for h in range(2):
-                square_x(0, h, True)
-            transpose_x(1, 1)
-            copy_and_square(1, 0, False)
-
             def weight_rows(m):
                 sign = -1.0 if m == 0 else 1.0
                 nc.vector.tensor_scalar(
@@ -367,31 +342,14 @@ def tile_dota_mix_pa_t_kernel(tc, x, gamma_class, mu, cur_var, pi, out):
                     in_=w_t[:].rearrange("p w t k -> p w k t"),
                 )
 
-            weight_rows(0)
-            weight_rows(1)
-            weight_rows_mu(0)
-            turn_weights(0)
-            weight_rows(2)
-            weight_rows_mu(1)
-            turn_weights(1)
-            transpose_x(2, 0)
-            weight_rows(3)
-            weight_rows_mu(2)
-            turn_weights(2)
-            quantise(0)
-            weight_rows_mu(3)
-            turn_weights(3)
-            copy_and_square(1, 1, True)
-            for n in range(WARM):
-                keep_busy()
-            for m in range(MODES):
+            def quantise_weights(m):
                 nc.vector.quantize_mx(
                     out=w_words[:, m, :, :].rearrange("p w k -> p (w k)").bitcast(FP8X4),
                     scales=w_scales[:, m, :, :].rearrange("p w k -> p (w k)"),
                     in_=w_grouped[:, m, :, :].rearrange("p w k -> p (w k)"),
                 )
-                if m >= 1:
-                    mx_group(0, m)
+
+            def sum_quad(m):
                 nc.vector.scalar_tensor_tensor(
                     out=inv_var[:, m, :],
                     in0=mu_sb[:, m, :],
@@ -401,99 +359,165 @@ def tile_dota_mix_pa_t_kernel(tc, x, gamma_class, mu, cur_var, pi, out):
                     op1=ALU.mult,
                     accum_out=quad[:, m : m + 1],
                 )
-                if m == 1:
-                    transpose_x(2, 1)
+
+            for n in range(WARM):
+                keep_busy()
+            for h in range(2):
+                transpose_x(0, h)
+                copy_x(0, h, True)
+            load_x(4)
+            weight_rows(0)
+            weight_rows(1)
+            weight_rows_mu(0)
+            turn_weights(0)
+            weight_rows(2)
+            weight_rows_mu(1)
+            turn_weights(1)
+            weight_rows(3)
+            weight_rows_mu(2)
+            turn_weights(2)
+            square_x(0, 0, True)
+            weight_rows_mu(3)
+            turn_weights(3)
+            square_x(0, 1, True)
+            for n in range(WARM2):
+                keep_busy()
+            transpose_x(1, 0)
+            copy_and_square(1, 0, False)
+            quantise(0)
+            quantise_weights(0)
+            quantise_weights(1)
+            mx_group(0, 1)
+            transpose_x(1, 1)
+            copy_and_square(1, 1, X1V)
+            load_x(5)
+            quantise_weights(2)
+            mx_group(0, 2)
+            transpose_x(2, 0)
+            copy_and_square(2, 0, False)
+            sum_quad(0)
+            quantise_weights(3)
+            mx_group(0, 3)
+            transpose_x(2, 1)
+            if not X2V:
+                copy_and_square(2, 1, False)
+            sum_quad(1)
+            sum_quad(2)
+            sum_quad(3)
+            quantise(1)
+            if X2V:
+                copy_x(2, 1, True)
             nc.vector.tensor_tensor(out=quad[:], in0=quad[:], in1=log_det[:], op=ALU.add)
+            transpose_x(3, 0)
+            copy_and_square(3, 0, False)
             nc.vector.scalar_tensor_tensor(
                 out=bias[:], in0=quad[:], scalar=-0.5, in1=ln_pi[:], op0=ALU.mult, op1=ALU.add
             )
+            if X2V:
+                square_x(2, 1, True)
             nc.vector.tensor_scalar(out=dbias[:], in0=bias[:], scalar1=bias[:, 0:1], scalar2=None, op0=ALU.subtract)
-            quantise(1)
-            copy_and_square(2, 0, False)
-            if RELU_S(0) and RO == 1:
-                first_max(0, False)
             for n in range(3, ACC_BANKS):
                 mx_group(n // 3, n % 3 + 1)
-            transpose_x(3, 0)
-            copy_and_square(2, 1, False)
+            first_max(0, True)
             transpose_x(3, 1)
-            if MO == 1:
-                if not RELU_S(0):
-                    first_max(0, True)
-                running_max(0, 2)
-                running_max(0, 3)
-            for h in range(2):
-                copy_and_square(3, h, False)
-            for i in range(2, QO):
-                quantise(i)
+            if not X3V:
+                copy_and_square(3, 1, False)
+            quantise(2)
+            if X3V:
+                copy_x(3, 1, True)
+            running_max(0, 2)
+            transpose_x(4, 0)
+            copy_and_square(4, 0, False)
+            if X3V:
+                square_x(3, 1, True)
+            running_max(0, 3)
+            transpose_x(4, 1)
+            copy_and_square(4, 1, X4V)
+            quantise(3)
 
         big = ctx.enter_context(tc.tile_pool(name="big", bufs=9))
         sums = ctx.enter_context(tc.tile_pool(name="sums", bufs=2))
 
         limit = 0
         t = -1
+        x_next = READY
+        x_turned = READY + (0 if PRE else 99)
+        q_next = READY - 1
+        loaded = READY + 1
         while state["done"] < len(units):
             t += 1
             banks = TURN_BANKS if t < BLOCKS else DRAIN_BANKS
             ln_group = LN_STEP.index(t) if t in LN_STEP else None
-            if is_block(t + AHEAD + 1):
-                load_x(t + AHEAD + 1)
+            xi = x_next if ln_group is None and x_next < BLOCKS else None
+            qi = q_next if q_next < min(x_next, BLOCKS) else None
+            if qi is not None:
+                q_next += 1
+            if ln_group is None:
+                if PRE and t == 0:
+                    transpose_x(READY, 0)
+                    x_turned += 1
+                x_next += 1
+            if loaded < BLOCKS and loaded <= x_next + 1:
+                load_x(loaded)
+                loaded += 1
             if t < GAMMA_LOADS:
                 load_gamma(t)
             count = PER_STEP(t)
             left = count
             order = ORDER(t)
             pump(banks)
-            for pos, k in enumerate(order):
-                if k == "a" and is_block(t + MO) and not RELU_S(t + MO):
-                    first_max(t + MO, True)
-                elif k == "r" and is_block(t + RO) and RELU_S(t + RO):
-                    first_max(t + RO, False)
-                elif k in "bc" and is_block(t + MO):
-                    running_max(t + MO, 2 + "bc".index(k))
+            for k in order:
+                if k == "a" and is_block(t + 1) and not RELU_S(t + 1):
+                    first_max(t + 1, True)
+                elif k == "r" and is_block(t + 1) and RELU_S(t + 1):
+                    first_max(t + 1, False)
+                elif k in "bc" and is_block(t + 1):
+                    running_max(t + 1, 2 + "bc".index(k))
                 elif k in "def":
                     q = "def".index(k)
                     if is_block(t):
                         subtract_max(t, q + 1)
                     n = 3 * t + q + ACC_BANKS
-                    if is_block(n // 3) and t >= 0:
+                    if is_block(n // 3):
                         mx_group(n // 3, n % 3 + 1)
-                elif k == "q" and is_block(t + QO):
-                    quantise(t + QO)
+                elif k == "q" and qi is not None:
+                    quantise(qi)
                 elif k == "u":
-                    if t >= BLOCKS and DUMMY and left % DUMMY == 0:
-                        keep_busy()
                     if left > 0:
                         left -= 1
                         next_unit(banks)
-                elif k in "yz" and is_block(t + AHEAD):
-                    transpose_x(t + AHEAD, "yz".index(k))
-                elif k in "YZ" and is_block(t + AHEAD):
+                elif k == "x" and x_turned < BLOCKS and x_turned == x_next and t + 1 not in LN_STEP:
+                    transpose_x(x_turned, 0)
+                    x_turned += 1
+                elif k == "z" and xi is not None:
+                    transpose_x(xi, 1)
+                elif k in "y" and xi is not None:
+                    transpose_x(xi, "yz".index(k))
+                elif k in "YZ" and xi is not None:
                     h = "YZ".index(k)
-                    if SQV(t + AHEAD, h):
-                        copy_x(t + AHEAD, h, False)
+                    if SQV(xi, h):
+                        copy_x(xi, h, False)
                     else:
-                        copy_and_square(t + AHEAD, h, XV(t + AHEAD, h))
-                elif k in "VW" and is_block(t + AHEAD - 1) and t >= 1:
+                        copy_and_square(xi, h, XV(xi, h))
+                elif k in "VW" and qi is not None and qi >= READY:
                     h = "VW".index(k)
-                    if SQV(t + AHEAD - 1, h):
-                        square_x(t + AHEAD - 1, h, True)
+                    if SQV(qi, h):
+                        square_x(qi, h, True)
                 elif k == "E" and is_block(t - 1):
                     exponentials(t - 1)
                 elif k == "G" and is_block(t - 1):
                     sum_modes(t - 1)
-                elif k == "L":
-                    if ln_group is not None:
-                        ln_sums(ln_group)
-                        limit = LAST_OF[ln_group] + 1
-                    while state["recip"] < limit and units.index(("r", state["recip"])) < state["done"] + 2 * count + 3:
+                elif k == "L" and ln_group is not None:
+                    for i in range(FIRST_OF[ln_group], LAST_OF[ln_group] + 1):
+                        ln_sum(i, "xt%d" % (i % XT_BANKS))
+                    limit = LAST_OF[ln_group] + 1
+                elif k == "P":
+                    while state["recip"] < limit and 4 * state["recip"] < state["done"] + 2 * count + LOOK:
                         reciprocal_sum(state["recip"])
                         state["recip"] += 1
             for n in range(left):
-                if t >= BLOCKS and DUMMY and (left - n) % DUMMY == 0:
-                    keep_busy()
                 next_unit(banks)
-            if t >= BLOCKS or t - 1 in LN_STEP or WAIT == 0:
-                state["avail"] = len(units) if limit == BLOCKS else units.index(("r", limit))
+            if t >= BLOCKS or t not in LN_STEP:
+                state["avail"] = 4 * state["recip"]
             if t >= BLOCKS:
                 pump(banks)

@@ -29,7 +29,7 @@ ACC_BANKS = 4
 XT_BANKS = 2
 LOOK = 2
 QSTEP = 2
-READY = 5
+READY = 4
 AHEAD = 5
 GROUPS = (4,4,4,3,1)
 GROUP_OF = [g for g, n in enumerate(GROUPS) for i in range(n)]
@@ -41,16 +41,19 @@ SCRAP = ["t1"]
 WARM = 4
 PRE = True
 WARM2 = 0
+X_LN1 = True
 X1V = False
-X2V = True
-X3V = True
+X2V = False
+X3V = False
 X4V = False
 RAT = 7
 DUMMY = 0
+DSTART = 14
+BURST = 0
 WAIT = 1
 TURN_BANKS = ("t0", "t1")
 WEIGHT_BANKS = ("t0", "t1", "p3", "p2")
-DRAIN_BANKS = ("t0", "t1", "p0", "p1", "p2", "p3")
+DRAIN_BANKS = ("p0", "p1", "p2", "p3")
 
 
 def XV(i, h):
@@ -58,7 +61,7 @@ def XV(i, h):
 
 
 def SQV(i, h):
-    return h == 1
+    return False
 
 
 def PER_STEP(t):
@@ -66,7 +69,7 @@ def PER_STEP(t):
 
 
 def RELU_S(t):
-    return t - 1 not in LN_STEP
+    return t - 1 not in LN_STEP and t > 4
 
 
 def VIA_S(i, jl):
@@ -74,7 +77,7 @@ def VIA_S(i, jl):
 
 
 def ORDER(t):
-    return "rdWauebEGLuqfcuxP" if t in LN_STEP else "rdWuYauebEGuzxuqfcuZP"
+    return "rdWzaeAbBEGLqCfDcuxP" if t == LN_STEP[0] else ("rdWauebEGLuqfcuxP" if t in LN_STEP else "rdWuYauebEGuzxuqfcuZP")
 
 
 def tile_dota_mix_pa_t_kernel(tc, x, gamma_class, mu, cur_var, pi, out):
@@ -119,7 +122,7 @@ def tile_dota_mix_pa_t_kernel(tc, x, gamma_class, mu, cur_var, pi, out):
             return 0 <= i < BLOCKS
 
         def keep_busy():
-            scrap = psum.tile([P, BLOCK], F32, tag=SCRAP[0], name="scrap")
+            scrap = psum.tile([P, BLOCK], F32, tag="xt1", name="scrap")
             nc.tensor.matmul(scrap[:], lhsT=idle[:, 0:P], rhs=idle[:], start=True, stop=True)
 
         def load_x(i):
@@ -152,12 +155,14 @@ def tile_dota_mix_pa_t_kernel(tc, x, gamma_class, mu, cur_var, pi, out):
 
         def square_x(i, h, on_vector):
             cols = slice(h * HALF, (h + 1) * HALF)
-            dst = grouped[i][:, 0, cols, :].rearrange("p c (u e) -> p c u e", e=2)
-            src = x_t[(i, h)][:].bitcast(BF16).rearrange("p u (c e) -> p c u e", e=2)
             if on_vector:
-                x_g = grouped[i][:, 1, cols, :].rearrange("p c (u e) -> p c u e", e=2)
-                nc.vector.tensor_tensor(out=dst, in0=src, in1=x_g, op=ALU.mult)
+                x_g = grouped[i][:, 1, cols, :].rearrange("p c t -> p (c t)")
+                nc.vector.tensor_tensor(
+                    out=grouped[i][:, 0, cols, :].rearrange("p c t -> p (c t)"), in0=x_g, in1=x_g, op=ALU.mult
+                )
             else:
+                dst = grouped[i][:, 0, cols, :].rearrange("p c (u e) -> p c u e", e=2)
+                src = x_t[(i, h)][:].bitcast(BF16).rearrange("p u (c e) -> p c u e", e=2)
                 nc.scalar.activation(out=dst, in_=src, func=ACT.Square)
 
         def copy_and_square(i, h, on_vector):
@@ -249,11 +254,13 @@ def tile_dota_mix_pa_t_kernel(tc, x, gamma_class, mu, cur_var, pi, out):
 
         units = [(i, jl) for i in range(BLOCKS) for jl in range(TILES_PER_BLOCK)]
         turned = {}
-        state = {"avail": 0, "turn": 0, "done": 0, "bank": 0, "recip": 0}
+        bank_of = {}
+        state = {"avail": 0, "turn": 0, "done": 0, "free": TURN_BANKS, "recip": 0}
 
-        def turn(n, banks):
-            bank = banks[state["bank"] % len(banks)]
-            state["bank"] += 1
+        def turn(n):
+            bank = state["free"][0]
+            state["free"] = state["free"][1:]
+            bank_of[n] = bank
             i, jl = units[n]
             turned[n] = psum.tile([P, MODES, CLASSES], F32, tag=bank, name="tb")
             for q in range(MODES):
@@ -274,16 +281,17 @@ def tile_dota_mix_pa_t_kernel(tc, x, gamma_class, mu, cur_var, pi, out):
                 nc.vector.tensor_tensor(out=dst, in0=src, in1=factor, op=ALU.mult)
             nc.sync.dma_start(out=out_rows[:, i * TILES_PER_BLOCK + jl, :], in_=result[i][:, jl, :])
 
-        def pump(banks):
-            while state["turn"] < state["avail"] and state["turn"] < state["done"] + len(banks):
-                turn(state["turn"], banks)
+        def pump():
+            while state["turn"] < state["avail"] and state["free"]:
+                turn(state["turn"])
                 state["turn"] += 1
 
-        def next_unit(banks):
+        def next_unit():
             if state["done"] < state["turn"]:
                 finish(state["done"])
+                state["free"] = state["free"] + (bank_of[state["done"]],)
                 state["done"] += 1
-                pump(banks)
+                pump()
 
         with tc.tile_pool(name="prep", bufs=1) as prep:
             var_sb = prep.tile([P, MODES, FEATURES], BF16, name="var_sb")
@@ -390,7 +398,6 @@ def tile_dota_mix_pa_t_kernel(tc, x, gamma_class, mu, cur_var, pi, out):
             mx_group(0, 1)
             transpose_x(1, 1)
             copy_and_square(1, 1, X1V)
-            load_x(5)
             quantise_weights(2)
             mx_group(0, 2)
             transpose_x(2, 0)
@@ -426,14 +433,9 @@ def tile_dota_mix_pa_t_kernel(tc, x, gamma_class, mu, cur_var, pi, out):
             if X3V:
                 copy_x(3, 1, True)
             running_max(0, 2)
-            transpose_x(4, 0)
-            copy_and_square(4, 0, False)
             if X3V:
                 square_x(3, 1, True)
             running_max(0, 3)
-            transpose_x(4, 1)
-            copy_and_square(4, 1, X4V)
-            quantise(3)
 
         big = ctx.enter_context(tc.tile_pool(name="big", bufs=9))
         sums = ctx.enter_context(tc.tile_pool(name="sums", bufs=2))
@@ -446,13 +448,15 @@ def tile_dota_mix_pa_t_kernel(tc, x, gamma_class, mu, cur_var, pi, out):
         loaded = READY + 1
         while state["done"] < len(units):
             t += 1
-            banks = TURN_BANKS if t < BLOCKS else DRAIN_BANKS
+            if t == BLOCKS:
+                state["free"] = state["free"] + DRAIN_BANKS
             ln_group = LN_STEP.index(t) if t in LN_STEP else None
-            xi = x_next if ln_group is None and x_next < BLOCKS else None
+            skip = ln_group is not None and not (X_LN1 and ln_group == 0)
+            xi = x_next if not skip and x_next < BLOCKS else None
             qi = q_next if q_next < min(x_next, BLOCKS) else None
             if qi is not None:
                 q_next += 1
-            if ln_group is None:
+            if not skip:
                 if PRE and t == 0:
                     transpose_x(READY, 0)
                     x_turned += 1
@@ -465,7 +469,7 @@ def tile_dota_mix_pa_t_kernel(tc, x, gamma_class, mu, cur_var, pi, out):
             count = PER_STEP(t)
             left = count
             order = ORDER(t)
-            pump(banks)
+            pump()
             for k in order:
                 if k == "a" and is_block(t + 1) and not RELU_S(t + 1):
                     first_max(t + 1, True)
@@ -485,14 +489,18 @@ def tile_dota_mix_pa_t_kernel(tc, x, gamma_class, mu, cur_var, pi, out):
                 elif k == "u":
                     if left > 0:
                         left -= 1
-                        next_unit(banks)
-                elif k == "x" and x_turned < BLOCKS and x_turned == x_next and t + 1 not in LN_STEP:
+                        next_unit()
+                elif k == "x" and x_turned < BLOCKS and x_turned == x_next and (t + 1 not in LN_STEP or (X_LN1 and t + 1 == LN_STEP[0])):
                     transpose_x(x_turned, 0)
                     x_turned += 1
                 elif k == "z" and xi is not None:
                     transpose_x(xi, 1)
                 elif k in "y" and xi is not None:
                     transpose_x(xi, "yz".index(k))
+                elif k in "AB" and xi is not None:
+                    copy_x(xi, "AB".index(k), True)
+                elif k in "CD" and xi is not None:
+                    square_x(xi, "CD".index(k), True)
                 elif k in "YZ" and xi is not None:
                     h = "YZ".index(k)
                     if SQV(xi, h):
@@ -509,15 +517,15 @@ def tile_dota_mix_pa_t_kernel(tc, x, gamma_class, mu, cur_var, pi, out):
                     sum_modes(t - 1)
                 elif k == "L" and ln_group is not None:
                     for i in range(FIRST_OF[ln_group], LAST_OF[ln_group] + 1):
-                        ln_sum(i, "xt%d" % (i % XT_BANKS))
+                        ln_sum(i, "t%d" % (i % 2) if X_LN1 and ln_group == 0 else "xt%d" % (i % XT_BANKS))
                     limit = LAST_OF[ln_group] + 1
                 elif k == "P":
                     while state["recip"] < limit and 4 * state["recip"] < state["done"] + 2 * count + LOOK:
                         reciprocal_sum(state["recip"])
                         state["recip"] += 1
             for n in range(left):
-                next_unit(banks)
+                next_unit()
             if t >= BLOCKS or t not in LN_STEP:
                 state["avail"] = 4 * state["recip"]
             if t >= BLOCKS:
-                pump(banks)
+                pump()

@@ -31,7 +31,7 @@ LOOK = 2
 QSTEP = 2
 READY = 4
 AHEAD = 5
-GROUPS = (4,4,4,3,1)
+GROUPS = (4,4,4,2,2)
 GROUP_OF = [g for g, n in enumerate(GROUPS) for i in range(n)]
 FIRST_OF = [sum(GROUPS[:g]) for g in range(len(GROUPS))]
 LAST_OF = [sum(GROUPS[: g + 1]) - 1 for g in range(len(GROUPS))]
@@ -40,6 +40,11 @@ LN_STEP = [last + 2 for last in LAST_OF]
 SCRAP = ["t1"]
 WARM = 4
 PRE = True
+PRE1 = True
+D1 = 2
+D2 = 1
+D3 = 1
+D4 = 1
 WARM2 = 0
 X_LN1 = True
 X1V = False
@@ -60,6 +65,10 @@ def XV(i, h):
     return False
 
 
+def CPV(i, h):
+    return False
+
+
 def SQV(i, h):
     return False
 
@@ -69,7 +78,7 @@ def PER_STEP(t):
 
 
 def RELU_S(t):
-    return t - 1 not in LN_STEP and t > 4
+    return t - 1 not in LN_STEP and t > 5
 
 
 def VIA_S(i, jl):
@@ -77,7 +86,7 @@ def VIA_S(i, jl):
 
 
 def ORDER(t):
-    return "rdWzaeAbBEGLqCfDcuxP" if t == LN_STEP[0] else ("rdWauebEGLuqfcuxP" if t in LN_STEP else "rdWuYauebEGuzxuqfcuZP")
+    return "rdWzaeAbBEGLqCfDcuxP" if t == LN_STEP[0] else ("rdWauebEGLuqfcuxP" if t in LN_STEP else "rduYauzebEGuxuqfcuZP")
 
 
 def tile_dota_mix_pa_t_kernel(tc, x, gamma_class, mu, cur_var, pi, out):
@@ -231,7 +240,8 @@ def tile_dota_mix_pa_t_kernel(tc, x, gamma_class, mu, cur_var, pi, out):
 
         def sum_modes(i):
             half_sums = two.tile([P, 2, BLOCK], F32, name="hs")
-            nc.gpsimd.tensor_tensor(out=half_sums[:], in0=expo[i][:, 0:2, :], in1=expo[i][:, 2:4, :], op=ALU.add)
+            for n in range(2):
+                nc.gpsimd.tensor_tensor(out=half_sums[:, n, :], in0=expo[i][:, n, :], in1=expo[i][:, n + 2, :], op=ALU.add)
             g = GROUP_OF[i]
             if i == FIRST_OF[g]:
                 esum[g] = sums.tile([P, max(GROUPS), BLOCK], F32, name="ssum")
@@ -374,13 +384,17 @@ def tile_dota_mix_pa_t_kernel(tc, x, gamma_class, mu, cur_var, pi, out):
                 transpose_x(0, h)
                 copy_x(0, h, True)
             load_x(4)
+            transpose_x(1, 0)
+            copy_and_square(1, 0, False)
             weight_rows(0)
             weight_rows(1)
             weight_rows_mu(0)
             turn_weights(0)
+            transpose_x(1, 1)
             weight_rows(2)
             weight_rows_mu(1)
             turn_weights(1)
+            transpose_x(2, 0)
             weight_rows(3)
             weight_rows_mu(2)
             turn_weights(2)
@@ -388,53 +402,37 @@ def tile_dota_mix_pa_t_kernel(tc, x, gamma_class, mu, cur_var, pi, out):
             weight_rows_mu(3)
             turn_weights(3)
             square_x(0, 1, True)
-            for n in range(WARM2):
-                keep_busy()
-            transpose_x(1, 0)
-            copy_and_square(1, 0, False)
+            copy_and_square(1, 1, False)
+            copy_and_square(2, 0, False)
             quantise(0)
             quantise_weights(0)
             quantise_weights(1)
             mx_group(0, 1)
-            transpose_x(1, 1)
-            copy_and_square(1, 1, X1V)
             quantise_weights(2)
+            transpose_x(2, 1)
             mx_group(0, 2)
-            transpose_x(2, 0)
-            copy_and_square(2, 0, False)
+            copy_and_square(2, 1, X2V)
             sum_quad(0)
             quantise_weights(3)
+            transpose_x(3, 0)
             mx_group(0, 3)
-            transpose_x(2, 1)
-            if not X2V:
-                copy_and_square(2, 1, False)
+            copy_and_square(3, 0, False)
             sum_quad(1)
+            quantise(1)
             sum_quad(2)
             sum_quad(3)
-            quantise(1)
-            if X2V:
-                copy_x(2, 1, True)
             nc.vector.tensor_tensor(out=quad[:], in0=quad[:], in1=log_det[:], op=ALU.add)
-            transpose_x(3, 0)
-            copy_and_square(3, 0, False)
             nc.vector.scalar_tensor_tensor(
                 out=bias[:], in0=quad[:], scalar=-0.5, in1=ln_pi[:], op0=ALU.mult, op1=ALU.add
             )
-            if X2V:
-                square_x(2, 1, True)
             nc.vector.tensor_scalar(out=dbias[:], in0=bias[:], scalar1=bias[:, 0:1], scalar2=None, op0=ALU.subtract)
+            transpose_x(3, 1)
             for n in range(3, ACC_BANKS):
                 mx_group(n // 3, n % 3 + 1)
             first_max(0, True)
-            transpose_x(3, 1)
-            if not X3V:
-                copy_and_square(3, 1, False)
+            copy_and_square(3, 1, X3V)
             quantise(2)
-            if X3V:
-                copy_x(3, 1, True)
             running_max(0, 2)
-            if X3V:
-                square_x(3, 1, True)
             running_max(0, 3)
 
         big = ctx.enter_context(tc.tile_pool(name="big", bufs=9))
@@ -460,6 +458,8 @@ def tile_dota_mix_pa_t_kernel(tc, x, gamma_class, mu, cur_var, pi, out):
                 if PRE and t == 0:
                     transpose_x(READY, 0)
                     x_turned += 1
+                    if PRE1:
+                        transpose_x(READY, 1)
                 x_next += 1
             if loaded < BLOCKS and loaded <= x_next + 1:
                 load_x(loaded)
@@ -493,7 +493,7 @@ def tile_dota_mix_pa_t_kernel(tc, x, gamma_class, mu, cur_var, pi, out):
                 elif k == "x" and x_turned < BLOCKS and x_turned == x_next and (t + 1 not in LN_STEP or (X_LN1 and t + 1 == LN_STEP[0])):
                     transpose_x(x_turned, 0)
                     x_turned += 1
-                elif k == "z" and xi is not None:
+                elif k == "z" and xi is not None and not (PRE1 and t == 0):
                     transpose_x(xi, 1)
                 elif k in "y" and xi is not None:
                     transpose_x(xi, "yz".index(k))
@@ -503,7 +503,10 @@ def tile_dota_mix_pa_t_kernel(tc, x, gamma_class, mu, cur_var, pi, out):
                     square_x(xi, "CD".index(k), True)
                 elif k in "YZ" and xi is not None:
                     h = "YZ".index(k)
-                    if SQV(xi, h):
+                    if CPV(xi, h):
+                        copy_x(xi, h, True)
+                        square_x(xi, h, False)
+                    elif SQV(xi, h):
                         copy_x(xi, h, False)
                     else:
                         copy_and_square(xi, h, XV(xi, h))

@@ -69,6 +69,14 @@ def CPV(i, h):
     return False
 
 
+def RV(i):
+    return False
+
+
+def SV(i):
+    return False
+
+
 def SQV(i, h):
     return False
 
@@ -78,7 +86,7 @@ def PER_STEP(t):
 
 
 def RELU_S(t):
-    return t - 1 not in LN_STEP and t > 5
+    return t - 1 not in LN_STEP and t > 7
 
 
 def VIA_S(i, jl):
@@ -86,7 +94,7 @@ def VIA_S(i, jl):
 
 
 def ORDER(t):
-    return "rdWzaeAbBEGLqCfDcuxP" if t == LN_STEP[0] else ("rdWauebEGLuqfcuxP" if t in LN_STEP else "rduYauzebEGuxuqfcuZP")
+    return "rdWzaeAbBEGLqCfDcuxP" if t == LN_STEP[0] else ("rdaEG!ue!b!uq!fcuxPL" if t in LN_STEP else "rduYauzebEGuxuqfcuZP")
 
 
 def tile_dota_mix_pa_t_kernel(tc, x, gamma_class, mu, cur_var, pi, out):
@@ -280,16 +288,17 @@ def tile_dota_mix_pa_t_kernel(tc, x, gamma_class, mu, cur_var, pi, out):
             i, jl = units[n]
             if jl == 0:
                 result[i] = outp.tile([P, TILES_PER_BLOCK, CLASSES * MODES], F32, name="o_sb")
-            dst = result[i][:, jl, :].rearrange("p (k m) -> p k m", m=MODES)
-            src = turned[n][:].rearrange("p m k -> p k m")
-            factor = ratio[i][:, jl, :].unsqueeze(2).to_broadcast([P, CLASSES, MODES])
-            if VIA_S(i, jl):
-                stage = stg.tile([P, CLASSES, MODES], F32, name="stage")
-                nc.scalar.copy(out=stage[:], in_=src)
-                nc.gpsimd.tensor_tensor(out=dst, in0=stage[:], in1=factor, op=ALU.mult)
-            else:
-                nc.vector.tensor_tensor(out=dst, in0=src, in1=factor, op=ALU.mult)
-            nc.sync.dma_start(out=out_rows[:, i * TILES_PER_BLOCK + jl, :], in_=result[i][:, jl, :])
+            parts = 2 if n == len(units) - 1 else 1
+            for c in range(parts):
+                ks = slice(c * CLASSES // parts, (c + 1) * CLASSES // parts)
+                cols = slice(c * CLASSES * MODES // parts, (c + 1) * CLASSES * MODES // parts)
+                nc.vector.tensor_tensor(
+                    out=result[i][:, jl, cols].rearrange("p (k m) -> p k m", m=MODES),
+                    in0=turned[n][:, :, ks].rearrange("p m k -> p k m"),
+                    in1=ratio[i][:, jl, ks].unsqueeze(2).to_broadcast([P, CLASSES // parts, MODES]),
+                    op=ALU.mult,
+                )
+                nc.sync.dma_start(out=out_rows[:, i * TILES_PER_BLOCK + jl, cols], in_=result[i][:, jl, cols])
 
         def pump():
             while state["turn"] < state["avail"] and state["free"]:
@@ -439,6 +448,7 @@ def tile_dota_mix_pa_t_kernel(tc, x, gamma_class, mu, cur_var, pi, out):
         sums = ctx.enter_context(tc.tile_pool(name="sums", bufs=2))
 
         limit = 0
+        ln_next = 0
         t = -1
         x_next = READY
         x_turned = READY + (0 if PRE else 99)
@@ -518,8 +528,9 @@ def tile_dota_mix_pa_t_kernel(tc, x, gamma_class, mu, cur_var, pi, out):
                     exponentials(t - 1)
                 elif k == "G" and is_block(t - 1):
                     sum_modes(t - 1)
-                elif k == "L" and ln_group is not None:
-                    for i in range(FIRST_OF[ln_group], LAST_OF[ln_group] + 1):
+                elif k in "L!" and ln_group is not None and ln_next < LAST_OF[ln_group] + 1:
+                    for i in range(ln_next, LAST_OF[ln_group] + 1 if k == "L" else ln_next + 1):
+                        ln_next = i + 1
                         ln_sum(i, "t%d" % (i % 2) if X_LN1 and ln_group == 0 else "xt%d" % (i % XT_BANKS))
                     limit = LAST_OF[ln_group] + 1
                 elif k == "P":

@@ -248,8 +248,7 @@ def tile_dota_mix_pa_t_kernel(tc, x, gamma_class, mu, cur_var, pi, out):
 
         def sum_modes(i):
             half_sums = two.tile([P, 2, BLOCK], F32, name="hs")
-            for n in range(2):
-                nc.gpsimd.tensor_tensor(out=half_sums[:, n, :], in0=expo[i][:, n, :], in1=expo[i][:, n + 2, :], op=ALU.add)
+            nc.gpsimd.tensor_tensor(out=half_sums[:], in0=expo[i][:, 0:2, :], in1=expo[i][:, 2:4, :], op=ALU.add)
             g = GROUP_OF[i]
             if i == FIRST_OF[g]:
                 esum[g] = sums.tile([P, max(GROUPS), BLOCK], F32, name="ssum")

@@ -22,79 +22,26 @@ TILES_PER_BLOCK = 4
 BLOCKS = TILES // TILES_PER_BLOCK
 BLOCK = TILES_PER_BLOCK * P
 HALF = BLOCK // 2
-GAMMA_LOADS = 4
 FLOPS = 2 * 2 * SAMPLES * CLASSES * MODES * FEATURES
 
-ACC_BANKS = 4
-XT_BANKS = 2
-LOOK = 2
-QSTEP = 2
-READY = 4
-AHEAD = 5
-GROUPS = (4,4,4,2,2)
-GROUP_OF = [g for g, n in enumerate(GROUPS) for i in range(n)]
-FIRST_OF = [sum(GROUPS[:g]) for g in range(len(GROUPS))]
-LAST_OF = [sum(GROUPS[: g + 1]) - 1 for g in range(len(GROUPS))]
-LN_STEP = [last + 2 for last in LAST_OF]
+GAMMA_LOADS = 4
+CLOSING_TILES = 8
+X_BEFORE = 4
+LN_GROUPS = (4, 4, 4, 2, 2)
+FIRST_OF = [sum(LN_GROUPS[:g]) for g in range(len(LN_GROUPS))]
+LAST_OF = [first + size - 1 for first, size in zip(FIRST_OF, LN_GROUPS)]
+GROUP_OF = [g for g, size in enumerate(LN_GROUPS) for i in range(size)]
+LN_STEPS = [last + 2 for last in LAST_OF]
+FIRST_MAX_ON_VECTOR = set(range(8)) | {step + 1 for step in LN_STEPS}
 
-SCRAP = ["t1"]
-WARM = 4
-PRE = True
-PRE1 = True
-D1 = 2
-D2 = 1
-D3 = 1
-D4 = 1
-WARM2 = 0
-X_LN1 = True
-X1V = False
-X2V = False
-X3V = False
-X4V = False
-RAT = 7
-DUMMY = 0
-DSTART = 14
-BURST = 0
-WAIT = 1
-TURN_BANKS = ("t0", "t1")
+GROUP_BANKS = ("p0", "p1", "p2", "p3")
+X_BANKS = ("xt0", "xt1")
+TILE_BANKS = ("t0", "t1")
 WEIGHT_BANKS = ("t0", "t1", "p3", "p2")
-DRAIN_BANKS = ("p0", "p1", "p2", "p3")
-
-
-def XV(i, h):
-    return False
-
-
-def CPV(i, h):
-    return False
-
-
-def RV(i):
-    return False
-
-
-def SV(i):
-    return False
-
-
-def SQV(i, h):
-    return False
-
-
-def PER_STEP(t):
-    return 4 if t < BLOCKS else 8
-
-
-def RELU_S(t):
-    return t - 1 not in LN_STEP and t > 7
-
-
-def VIA_S(i, jl):
-    return False
-
-
-def ORDER(t):
-    return "rdWzaeAbBEGLqCfDcuxP" if t == LN_STEP[0] else ("rdaEG!ue!b!uq!fcuxPL" if t in LN_STEP else "rduYauzebEGuxuqfcuZP")
+WARM_BANK = "xt1"
+WARM_PASSES = 4
+CLOSING_WARM_BANK = "p2"
+TENSOR_SUMS = {BLOCKS - 1}
 
 
 def tile_dota_mix_pa_t_kernel(tc, x, gamma_class, mu, cur_var, pi, out):
@@ -109,15 +56,14 @@ def tile_dota_mix_pa_t_kernel(tc, x, gamma_class, mu, cur_var, pi, out):
         xin = ctx.enter_context(tc.tile_pool(name="xin", bufs=4))
         grp = ctx.enter_context(tc.tile_pool(name="grp", bufs=3))
         cod = ctx.enter_context(tc.tile_pool(name="cod", bufs=5))
-        two = ctx.enter_context(tc.tile_pool(name="two", bufs=2))
+        half = ctx.enter_context(tc.tile_pool(name="half", bufs=2))
         tops = ctx.enter_context(tc.tile_pool(name="tops", bufs=5))
-        rat = ctx.enter_context(tc.tile_pool(name="rat", bufs=RAT))
+        rat = ctx.enter_context(tc.tile_pool(name="rat", bufs=7))
         outp = ctx.enter_context(tc.tile_pool(name="outp", bufs=3))
-        stg = ctx.enter_context(tc.tile_pool(name="stg", bufs=2))
         psum = ctx.enter_context(tc.psum_pool(name="psum", bufs=1))
 
         identity = const.tile([P, P], F32, name="identf")
-        idle = const.tile([P, BLOCK], BF16, name="idle")
+        zeros = const.tile([P, BLOCK], BF16, name="zeros")
         identity_bf = const.tile([P, P], BF16, name="identb")
         w_words = const.tile([P, MODES, 2, CLASSES], U32, name="wq", align_bytes=64)
         w_scales = const.tile([P, MODES, 2, CLASSES], U8, name="ws", align_bytes=64)
@@ -127,20 +73,19 @@ def tile_dota_mix_pa_t_kernel(tc, x, gamma_class, mu, cur_var, pi, out):
         x_sb = {}
         x_t = {}
         grouped = {}
-        codes = {}
+        operands = {}
         group_acc = {}
         top = {}
         expo = {}
         esum = {}
+        sum_t = {}
         ratio = {}
+        expo_t = {}
         result = {}
 
         def is_block(i):
             return 0 <= i < BLOCKS
 
-        def keep_busy():
-            scrap = psum.tile([P, BLOCK], F32, tag="xt1", name="scrap")
-            nc.tensor.matmul(scrap[:], lhsT=idle[:, 0:P], rhs=idle[:], start=True, stop=True)
 
         def load_x(i):
             x_sb[i] = xin.tile([P, TILES_PER_BLOCK, FEATURES], BF16, name="x_sb")
@@ -151,7 +96,7 @@ def tile_dota_mix_pa_t_kernel(tc, x, gamma_class, mu, cur_var, pi, out):
             nc.sync.dma_start(out=gamma_sb[:, js, :], in_=gamma_rows[:, js, :])
 
         def transpose_x(i, h):
-            x_t[(i, h)] = psum.tile([P, 2, HALF], F32, tag="xt%d" % (h % XT_BANKS), name="xt")
+            x_t[(i, h)] = psum.tile([P, 2, HALF], F32, tag=X_BANKS[h], name="xt")
             pairs = x_sb[i][:].bitcast(F32)
             for jj in range(2):
                 for u in range(2):
@@ -162,8 +107,7 @@ def tile_dota_mix_pa_t_kernel(tc, x, gamma_class, mu, cur_var, pi, out):
         def copy_x(i, h, on_vector):
             if i not in grouped:
                 grouped[i] = grp.tile([P, 2, BLOCK, PACK], BF16, name="xg", align_bytes=64)
-            cols = slice(h * HALF, (h + 1) * HALF)
-            dst = grouped[i][:, 1, cols, :].bitcast(F32)
+            dst = grouped[i][:, 1, h * HALF : (h + 1) * HALF, :].bitcast(F32)
             src = x_t[(i, h)][:].rearrange("p u c -> p c u")
             if on_vector:
                 nc.vector.tensor_copy(out=dst, in_=src)
@@ -171,145 +115,184 @@ def tile_dota_mix_pa_t_kernel(tc, x, gamma_class, mu, cur_var, pi, out):
                 nc.scalar.copy(out=dst, in_=src)
 
         def square_x(i, h, on_vector):
-            cols = slice(h * HALF, (h + 1) * HALF)
+            xx_half = grouped[i][:, 0, h * HALF : (h + 1) * HALF, :]
             if on_vector:
-                x_g = grouped[i][:, 1, cols, :].rearrange("p c t -> p (c t)")
+                x_half = grouped[i][:, 1, h * HALF : (h + 1) * HALF, :].rearrange("p c t -> p (c t)")
                 nc.vector.tensor_tensor(
-                    out=grouped[i][:, 0, cols, :].rearrange("p c t -> p (c t)"), in0=x_g, in1=x_g, op=ALU.mult
+                    out=xx_half.rearrange("p c t -> p (c t)"), in0=x_half, in1=x_half, op=ALU.mult
                 )
             else:
-                dst = grouped[i][:, 0, cols, :].rearrange("p c (u e) -> p c u e", e=2)
-                src = x_t[(i, h)][:].bitcast(BF16).rearrange("p u (c e) -> p c u e", e=2)
-                nc.scalar.activation(out=dst, in_=src, func=ACT.Square)
+                nc.scalar.activation(
+                    out=xx_half.rearrange("p c (u e) -> p c u e", e=2),
+                    in_=x_t[(i, h)][:].bitcast(BF16).rearrange("p u (c e) -> p c u e", e=2),
+                    func=ACT.Square,
+                )
 
-        def copy_and_square(i, h, on_vector):
-            copy_x(i, h, on_vector)
-            square_x(i, h, on_vector)
+        def copy_and_square(i, h):
+            copy_x(i, h, False)
+            square_x(i, h, False)
 
-        def quantise(i):
+        def quantise_x(i):
             words = cod.tile([P, 2, BLOCK], U32, name="xq", align_bytes=64)
             scales = cod.tile([P, 2, BLOCK], U8, name="xs", align_bytes=64)
-            codes[i] = (words, scales)
+            operands[i] = (words, scales)
             nc.vector.quantize_mx(
                 out=words[:].rearrange("p w c -> p (w c)").bitcast(FP8X4),
                 scales=scales[:].rearrange("p w c -> p (w c)"),
                 in_=grouped[i][:].rearrange("p w c t -> p (w c t)"),
             )
 
-        def mx_group(i, m):
-            group_acc[(i, m)] = psum.tile([P, BLOCK], F32, tag="p%d" % ((3 * i + m - 1) % ACC_BANKS), name="acc")
-            words, scales = codes[i]
+
+        def mx_group(n):
+            i, m = n // 3, n % 3 + 1
+            group_acc[(i, m)] = psum.tile([P, BLOCK], F32, tag=GROUP_BANKS[n % len(GROUP_BANKS)], name="acc")
+            words, scales = operands[i]
             passes = ((0, m), (0, 0), (1, m), (1, 0))
-            for n, (w, mode) in enumerate(passes):
+            for s, (w, mode) in enumerate(passes):
                 nc.tensor.matmul_mx(
                     out=group_acc[(i, m)][:],
                     lhsT=w_words[:, mode, w, :].bitcast(FP8X4),
                     lhsT_scale=w_scales[:, mode, w, :],
                     rhs=words[:, w, :].bitcast(FP8X4),
                     rhs_scale=scales[:, w, :],
-                    start=(n == 0),
-                    stop=(n == len(passes) - 1),
+                    start=(s == 0),
+                    stop=(s == len(passes) - 1),
                 )
 
-        def first_max(i, on_vector):
+        def first_max(i):
             top[i] = tops.tile([P, BLOCK], F32, name="top")
-            if on_vector:
+            if i in FIRST_MAX_ON_VECTOR:
                 nc.vector.tensor_scalar(
                     out=top[i][:], in0=group_acc[(i, 1)][:], scalar1=dbias[:, 1:2], scalar2=0.0, op0=ALU.add, op1=ALU.max
                 )
-                return
-            nc.scalar.activation(out=top[i][:], in_=group_acc[(i, 1)][:], func=ACT.Relu, bias=dbias[:, 1:2])
+            else:
+                nc.scalar.activation(out=top[i][:], in_=group_acc[(i, 1)][:], func=ACT.Relu, bias=dbias[:, 1:2])
 
         def running_max(i, m):
-            nc.vector.scalar_tensor_tensor(
-                out=top[i][:],
-                in0=group_acc[(i, m)][:],
-                scalar=dbias[:, m : m + 1],
-                in1=top[i][:],
-                op0=ALU.add,
-                op1=ALU.max,
-            )
+            if is_block(i):
+                nc.vector.scalar_tensor_tensor(
+                    out=top[i][:],
+                    in0=group_acc[(i, m)][:],
+                    scalar=dbias[:, m : m + 1],
+                    in1=top[i][:],
+                    op0=ALU.add,
+                    op1=ALU.max,
+                )
 
         def subtract_max(i, m):
-            if m == 1:
-                expo[i] = big.tile([P, MODES, BLOCK], F32, name="de")
-            nc.vector.scalar_tensor_tensor(
-                out=expo[i][:, m, :],
-                in0=group_acc[(i, m)][:],
-                scalar=dbias[:, m : m + 1],
-                in1=top[i][:],
-                op0=ALU.add,
-                op1=ALU.subtract,
-            )
+            if is_block(i):
+                if m == 1:
+                    expo[i] = big.tile([P, MODES, BLOCK], F32, name="de")
+                nc.vector.scalar_tensor_tensor(
+                    out=expo[i][:, m, :],
+                    in0=group_acc[(i, m)][:],
+                    scalar=dbias[:, m : m + 1],
+                    in1=top[i][:],
+                    op0=ALU.add,
+                    op1=ALU.subtract,
+                )
+            following = 3 * i + m - 1 + len(GROUP_BANKS)
+            if is_block(following // 3):
+                mx_group(following)
+            elif is_block(i):
+                bank = GROUP_BANKS[following % len(GROUP_BANKS)]
+                if bank != CLOSING_WARM_BANK:
+                    line["banks"] = line["banks"] + (bank,)
+                    turn_tiles()
 
-        def exponentials(i):
-            nc.scalar.activation(out=expo[i][:, 0, :], in_=top[i][:], func=ACT.Exp, scale=-1.0)
-            nc.scalar.activation(out=expo[i][:, 1:4, :], in_=expo[i][:, 1:4, :], func=ACT.Exp)
+        def exponentials_and_sum(i):
+            if is_block(i):
+                nc.scalar.activation(out=expo[i][:, 0, :], in_=top[i][:], func=ACT.Exp, scale=-1.0)
+                nc.scalar.activation(out=expo[i][:, 1:4, :], in_=expo[i][:, 1:4, :], func=ACT.Exp)
+            if is_block(i) and i not in TENSOR_SUMS:
+                half_sums = half.tile([P, 2, BLOCK], F32, name="hs")
+                nc.gpsimd.tensor_tensor(
+                    out=half_sums[:], in0=expo[i][:, 0:2, :], in1=expo[i][:, 2:4, :], op=ALU.add
+                )
+                g = GROUP_OF[i]
+                if i == FIRST_OF[g]:
+                    esum[g] = sums.tile([P, max(LN_GROUPS), BLOCK], F32, name="ssum")
+                nc.gpsimd.tensor_tensor(
+                    out=esum[g][:, i - FIRST_OF[g], :], in0=half_sums[:, 0, :], in1=half_sums[:, 1, :], op=ALU.add
+                )
 
-        def sum_modes(i):
-            half_sums = two.tile([P, 2, BLOCK], F32, name="hs")
-            nc.gpsimd.tensor_tensor(out=half_sums[:], in0=expo[i][:, 0:2, :], in1=expo[i][:, 2:4, :], op=ALU.add)
-            g = GROUP_OF[i]
-            if i == FIRST_OF[g]:
-                esum[g] = sums.tile([P, max(GROUPS), BLOCK], F32, name="ssum")
-            nc.gpsimd.tensor_tensor(
-                out=esum[g][:, i - FIRST_OF[g], :], in0=half_sums[:, 0, :], in1=half_sums[:, 1, :], op=ALU.add
-            )
 
-        def ln_sum(i, bank):
-            s_t = psum.tile([P, TILES_PER_BLOCK, CLASSES], F32, tag=bank, name="st")
+        def turn_sum(i, bank):
+            sum_t[i] = psum.tile([P, TILES_PER_BLOCK, CLASSES], F32, tag=bank, name="st")
             g = GROUP_OF[i]
             for jl in range(TILES_PER_BLOCK):
-                nc.tensor.transpose(s_t[:, jl, :], esum[g][:, i - FIRST_OF[g], jl * P : (jl + 1) * P], identity[:])
+                cols = slice(jl * P, (jl + 1) * P)
+                terms = (
+                    [expo[i][:, m, cols] for m in range(MODES)]
+                    if i in TENSOR_SUMS
+                    else [esum[g][:, i - FIRST_OF[g], cols]]
+                )
+                for n, term in enumerate(terms):
+                    nc.tensor.matmul(
+                        sum_t[i][:, jl, :],
+                        lhsT=term,
+                        rhs=identity[:],
+                        start=(n == 0),
+                        stop=(n == len(terms) - 1),
+                        is_transpose=True,
+                    )
+
+        def ln_sum(i, bank):
+            if i not in sum_t:
+                turn_sum(i, bank)
             ratio[i] = rat.tile([P, TILES_PER_BLOCK, CLASSES], F32, name="rr")
-            nc.scalar.activation(out=ratio[i][:], in_=s_t[:], func=ACT.Ln)
+            nc.scalar.activation(out=ratio[i][:], in_=sum_t[i][:], func=ACT.Ln)
 
-        def reciprocal_sum(i):
-            nc.scalar.activation(out=ratio[i][:], in_=ratio[i][:], func=ACT.Exp, scale=-1.0)
-            js = slice(i * TILES_PER_BLOCK, (i + 1) * TILES_PER_BLOCK)
-            nc.gpsimd.tensor_tensor(out=ratio[i][:], in0=ratio[i][:], in1=gamma_sb[:, js, :], op=ALU.mult)
+        def warm(bank):
+            unread = psum.tile([P, BLOCK], F32, tag=bank, name="scrap")
+            nc.tensor.matmul(unread[:], lhsT=zeros[:, 0:P], rhs=zeros[:], start=True, stop=True)
 
-        units = [(i, jl) for i in range(BLOCKS) for jl in range(TILES_PER_BLOCK)]
-        turned = {}
+        line = {"divided": 0, "released": 0, "turned": 0, "finished": 0, "banks": TILE_BANKS}
         bank_of = {}
-        state = {"avail": 0, "turn": 0, "done": 0, "free": TURN_BANKS, "recip": 0}
 
-        def turn(n):
-            bank = state["free"][0]
-            state["free"] = state["free"][1:]
-            bank_of[n] = bank
-            i, jl = units[n]
-            turned[n] = psum.tile([P, MODES, CLASSES], F32, tag=bank, name="tb")
-            for q in range(MODES):
-                nc.tensor.transpose(turned[n][:, q, :], expo[i][:, q, jl * P : (jl + 1) * P], identity[:])
+        def divide_gamma(ln_blocks, per_step):
+            while (
+                line["divided"] < ln_blocks
+                and TILES_PER_BLOCK * line["divided"] < line["finished"] + 2 * per_step + 2
+            ):
+                i = line["divided"]
+                nc.scalar.activation(out=ratio[i][:], in_=ratio[i][:], func=ACT.Exp, scale=-1.0)
+                js = slice(i * TILES_PER_BLOCK, (i + 1) * TILES_PER_BLOCK)
+                nc.gpsimd.tensor_tensor(out=ratio[i][:], in0=ratio[i][:], in1=gamma_sb[:, js, :], op=ALU.mult)
+                line["divided"] += 1
 
-        def finish(n):
-            i, jl = units[n]
+        def turn_tiles():
+            while line["turned"] < line["released"] and line["banks"]:
+                j = line["turned"]
+                i, jl = divmod(j, TILES_PER_BLOCK)
+                bank_of[j] = line["banks"][0]
+                line["banks"] = line["banks"][1:]
+                expo_t[j] = psum.tile([P, MODES, CLASSES], F32, tag=bank_of[j], name="tb")
+                for m in range(MODES):
+                    nc.tensor.transpose(expo_t[j][:, m, :], expo[i][:, m, jl * P : (jl + 1) * P], identity[:])
+                line["turned"] += 1
+
+        def finish_tile():
+            j = line["finished"]
+            if j == line["turned"]:
+                return
+            i, jl = divmod(j, TILES_PER_BLOCK)
             if jl == 0:
                 result[i] = outp.tile([P, TILES_PER_BLOCK, CLASSES * MODES], F32, name="o_sb")
-            parts = 2 if n == len(units) - 1 else 1
+            parts = 2 if j == TILES - 1 else 1
             for c in range(parts):
                 ks = slice(c * CLASSES // parts, (c + 1) * CLASSES // parts)
                 cols = slice(c * CLASSES * MODES // parts, (c + 1) * CLASSES * MODES // parts)
                 nc.vector.tensor_tensor(
                     out=result[i][:, jl, cols].rearrange("p (k m) -> p k m", m=MODES),
-                    in0=turned[n][:, :, ks].rearrange("p m k -> p k m"),
+                    in0=expo_t[j][:, :, ks].rearrange("p m k -> p k m"),
                     in1=ratio[i][:, jl, ks].unsqueeze(2).to_broadcast([P, CLASSES // parts, MODES]),
                     op=ALU.mult,
                 )
-                nc.sync.dma_start(out=out_rows[:, i * TILES_PER_BLOCK + jl, cols], in_=result[i][:, jl, cols])
-
-        def pump():
-            while state["turn"] < state["avail"] and state["free"]:
-                turn(state["turn"])
-                state["turn"] += 1
-
-        def next_unit():
-            if state["done"] < state["turn"]:
-                finish(state["done"])
-                state["free"] = state["free"] + (bank_of[state["done"]],)
-                state["done"] += 1
-                pump()
+                nc.sync.dma_start(out=out_rows[:, j, cols], in_=result[i][:, jl, cols])
+            line["banks"] = line["banks"] + (bank_of[j],)
+            line["finished"] += 1
+            turn_tiles()
 
         with tc.tile_pool(name="prep", bufs=1) as prep:
             var_sb = prep.tile([P, MODES, FEATURES], BF16, name="var_sb")
@@ -320,9 +303,9 @@ def tile_dota_mix_pa_t_kernel(tc, x, gamma_class, mu, cur_var, pi, out):
                 nc.sync.dma_start(out=var_sb[:, m, :], in_=cur_var[:, m, :])
             load_x(0)
             nc.sync.dma_start(out=mu_sb[:], in_=mu)
-            for i in range(1, 4):
+            for i in range(1, X_BEFORE):
                 load_x(i)
-            nc.vector.memset(idle[:], 0.0)
+            nc.vector.memset(zeros[:], 0.0)
             make_identity(nc, identity[:])
             nc.gpsimd.tensor_copy(out=identity_bf[:], in_=identity[:])
 
@@ -346,16 +329,23 @@ def tile_dota_mix_pa_t_kernel(tc, x, gamma_class, mu, cur_var, pi, out):
             for m in range(MODES):
                 nc.scalar.activation(out=inv_var[:, m, :], in_=ln_var[:, m, :], func=ACT.Exp, scale=-1.0)
 
-            def weight_rows(m):
-                sign = -1.0 if m == 0 else 1.0
+            def sign(m):
+                return -1.0 if m == 0 else 1.0
+
+            def weigh(m):
                 nc.vector.tensor_scalar(
-                    out=w_rows[:, m, 0, :], in0=inv_var[:, m, :], scalar1=-0.5 * sign, scalar2=None, op0=ALU.mult
+                    out=w_rows[:, m, 0, :], in0=inv_var[:, m, :], scalar1=-0.5 * sign(m), scalar2=None, op0=ALU.mult
                 )
                 nc.vector.scalar_tensor_tensor(
-                    out=mu_iv[:, m, :], in0=mu_sb[:, m, :], scalar=sign, in1=inv_var[:, m, :], op0=ALU.mult, op1=ALU.mult
+                    out=mu_iv[:, m, :],
+                    in0=mu_sb[:, m, :],
+                    scalar=sign(m),
+                    in1=inv_var[:, m, :],
+                    op0=ALU.mult,
+                    op1=ALU.mult,
                 )
 
-            def weight_rows_mu(m):
+            def round_mu_iv(m):
                 nc.vector.tensor_copy(out=w_rows[:, m, 1, :], in_=mu_iv[:, m, :])
 
             def turn_weights(m):
@@ -379,54 +369,55 @@ def tile_dota_mix_pa_t_kernel(tc, x, gamma_class, mu, cur_var, pi, out):
                 nc.vector.scalar_tensor_tensor(
                     out=inv_var[:, m, :],
                     in0=mu_sb[:, m, :],
-                    scalar=-1.0 if m == 0 else 1.0,
+                    scalar=sign(m),
                     in1=mu_iv[:, m, :],
                     op0=ALU.mult,
                     op1=ALU.mult,
                     accum_out=quad[:, m : m + 1],
                 )
 
-            for n in range(WARM):
-                keep_busy()
+            for n in range(WARM_PASSES):
+                warm(WARM_BANK)
+
             for h in range(2):
                 transpose_x(0, h)
                 copy_x(0, h, True)
-            load_x(4)
+            load_x(X_BEFORE)
             transpose_x(1, 0)
-            copy_and_square(1, 0, False)
-            weight_rows(0)
-            weight_rows(1)
-            weight_rows_mu(0)
+            copy_and_square(1, 0)
+            weigh(0)
+            weigh(1)
+            round_mu_iv(0)
             turn_weights(0)
             transpose_x(1, 1)
-            weight_rows(2)
-            weight_rows_mu(1)
+            weigh(2)
+            round_mu_iv(1)
             turn_weights(1)
             transpose_x(2, 0)
-            weight_rows(3)
-            weight_rows_mu(2)
+            weigh(3)
+            round_mu_iv(2)
             turn_weights(2)
             square_x(0, 0, True)
-            weight_rows_mu(3)
+            round_mu_iv(3)
             turn_weights(3)
             square_x(0, 1, True)
-            copy_and_square(1, 1, False)
-            copy_and_square(2, 0, False)
-            quantise(0)
+            copy_and_square(1, 1)
+            copy_and_square(2, 0)
+            quantise_x(0)
             quantise_weights(0)
             quantise_weights(1)
-            mx_group(0, 1)
+            mx_group(0)
             quantise_weights(2)
             transpose_x(2, 1)
-            mx_group(0, 2)
-            copy_and_square(2, 1, X2V)
+            mx_group(1)
+            copy_and_square(2, 1)
             sum_quad(0)
             quantise_weights(3)
             transpose_x(3, 0)
-            mx_group(0, 3)
-            copy_and_square(3, 0, False)
+            mx_group(2)
+            copy_and_square(3, 0)
             sum_quad(1)
-            quantise(1)
+            quantise_x(1)
             sum_quad(2)
             sum_quad(3)
             nc.vector.tensor_tensor(out=quad[:], in0=quad[:], in1=log_det[:], op=ALU.add)
@@ -435,110 +426,164 @@ def tile_dota_mix_pa_t_kernel(tc, x, gamma_class, mu, cur_var, pi, out):
             )
             nc.vector.tensor_scalar(out=dbias[:], in0=bias[:], scalar1=bias[:, 0:1], scalar2=None, op0=ALU.subtract)
             transpose_x(3, 1)
-            for n in range(3, ACC_BANKS):
-                mx_group(n // 3, n % 3 + 1)
-            first_max(0, True)
-            copy_and_square(3, 1, X3V)
-            quantise(2)
+            mx_group(3)
+            first_max(0)
+            copy_and_square(3, 1)
+            quantise_x(2)
             running_max(0, 2)
             running_max(0, 3)
 
         big = ctx.enter_context(tc.tile_pool(name="big", bufs=9))
         sums = ctx.enter_context(tc.tile_pool(name="sums", bufs=2))
 
-        limit = 0
-        ln_next = 0
-        t = -1
-        x_next = READY
-        x_turned = READY + (0 if PRE else 99)
-        q_next = READY - 1
-        loaded = READY + 1
-        while state["done"] < len(units):
-            t += 1
-            if t == BLOCKS:
-                state["free"] = state["free"] + DRAIN_BANKS
-            ln_group = LN_STEP.index(t) if t in LN_STEP else None
-            skip = ln_group is not None and not (X_LN1 and ln_group == 0)
-            xi = x_next if not skip and x_next < BLOCKS else None
-            qi = q_next if q_next < min(x_next, BLOCKS) else None
-            if qi is not None:
-                q_next += 1
-            if not skip:
-                if PRE and t == 0:
-                    transpose_x(READY, 0)
-                    x_turned += 1
-                    if PRE1:
-                        transpose_x(READY, 1)
-                x_next += 1
-            if loaded < BLOCKS and loaded <= x_next + 1:
-                load_x(loaded)
-                loaded += 1
+        queue = {"loaded": X_BEFORE + 1, "prepared": X_BEFORE, "quantised": X_BEFORE - 1, "ln_blocks": 0}
+        for h in range(2):
+            transpose_x(X_BEFORE, h)
+
+        def transpose_next_x(t):
+            if is_block(queue["prepared"]) and (t + 1 not in LN_STEPS or t + 1 == LN_STEPS[0]):
+                transpose_x(queue["prepared"], 0)
+
+        def first_max_ahead(t, on_vector):
+            if is_block(t + 1) and (t + 1 in FIRST_MAX_ON_VECTOR) == on_vector:
+                first_max(t + 1)
+
+        def ordinary_step(t, x_block, q_block):
+            first_max_ahead(t, False)
+            subtract_max(t, 1)
+            finish_tile()
+            if x_block is not None:
+                copy_and_square(x_block, 0)
+            first_max_ahead(t, True)
+            finish_tile()
+            if x_block is not None and x_block > X_BEFORE:
+                transpose_x(x_block, 1)
+            subtract_max(t, 2)
+            running_max(t + 1, 2)
+            exponentials_and_sum(t - 1)
+            finish_tile()
+            transpose_next_x(t)
+            finish_tile()
+            if q_block is not None:
+                quantise_x(q_block)
+            subtract_max(t, 3)
+            running_max(t + 1, 3)
+            if x_block is not None:
+                copy_and_square(x_block, 1)
+            divide_gamma(queue["ln_blocks"], TILES_PER_BLOCK)
+
+        def first_ln_step(t, x_block, q_block):
+            first_max_ahead(t, False)
+            subtract_max(t, 1)
+            transpose_x(x_block, 1)
+            first_max_ahead(t, True)
+            subtract_max(t, 2)
+            copy_x(x_block, 0, True)
+            running_max(t + 1, 2)
+            copy_x(x_block, 1, True)
+            quantise_x(q_block)
+            exponentials_and_sum(t - 1)
+            for i in range(FIRST_OF[0], LAST_OF[0] + 1):
+                ln_sum(i, TILE_BANKS[i % 2])
+            square_x(x_block, 0, True)
+            subtract_max(t, 3)
+            square_x(x_block, 1, True)
+            running_max(t + 1, 3)
+            transpose_next_x(t)
+            queue["ln_blocks"] = LAST_OF[0] + 1
+            divide_gamma(queue["ln_blocks"], TILES_PER_BLOCK)
+
+        def ln_step(t, g, q_block):
+            def next_ln_sum(k):
+                i = FIRST_OF[g] + k
+                if i <= LAST_OF[g]:
+                    ln_sum(i, X_BANKS[i % 2])
+
+            first_max_ahead(t, False)
+            subtract_max(t, 1)
+            first_max_ahead(t, True)
+            exponentials_and_sum(t - 1)
+            next_ln_sum(0)
+            finish_tile()
+            subtract_max(t, 2)
+            next_ln_sum(1)
+            running_max(t + 1, 2)
+            next_ln_sum(2)
+            finish_tile()
+            if q_block is not None:
+                quantise_x(q_block)
+            next_ln_sum(3)
+            subtract_max(t, 3)
+            running_max(t + 1, 3)
+            if t == BLOCKS - 1:
+                for n in range(2):
+                    warm(CLOSING_WARM_BANK)
+            finish_tile()
+            transpose_next_x(t)
+            queue["ln_blocks"] = LAST_OF[g] + 1
+            divide_gamma(queue["ln_blocks"], TILES_PER_BLOCK if t < BLOCKS - 1 else CLOSING_TILES)
+            finish_tile()
+
+        def warm_and_finish(n):
+            for k in range(n):
+                warm(CLOSING_WARM_BANK)
+                finish_tile()
+
+        def release_all(blocks):
+            line["released"] = TILES_PER_BLOCK * blocks
+            turn_tiles()
+
+        def first_closing_step(t):
+            warm_and_finish(2)
+            exponentials_and_sum(t - 1)
+            release_all(BLOCKS)
+            warm_and_finish(3)
+            turn_sum(BLOCKS - 2, X_BANKS[0])
+            divide_gamma(queue["ln_blocks"], CLOSING_TILES)
+            warm_and_finish(3)
+            turn_sum(BLOCKS - 1, X_BANKS[1])
+
+        def closing_step(t):
+            if t in LN_STEPS:
+                for i in range(FIRST_OF[-1], BLOCKS):
+                    ln_sum(i, X_BANKS[i % 2])
+                queue["ln_blocks"] = BLOCKS
+            for n in range(3):
+                finish_tile()
+            divide_gamma(queue["ln_blocks"], CLOSING_TILES)
+            for n in range(CLOSING_TILES - 3):
+                finish_tile()
+
+        t = 0
+        while line["finished"] < TILES:
+            first_ln = t == LN_STEPS[0]
+            x_block = None
+            q_block = None
+            if queue["quantised"] < min(queue["prepared"], BLOCKS):
+                q_block = queue["quantised"]
+                queue["quantised"] += 1
+            if first_ln or t not in LN_STEPS:
+                if is_block(queue["prepared"]):
+                    x_block = queue["prepared"]
+                queue["prepared"] += 1
+            if is_block(queue["loaded"]) and queue["loaded"] <= queue["prepared"] + 1:
+                load_x(queue["loaded"])
+                queue["loaded"] += 1
             if t < GAMMA_LOADS:
                 load_gamma(t)
-            count = PER_STEP(t)
-            left = count
-            order = ORDER(t)
-            pump()
-            for k in order:
-                if k == "a" and is_block(t + 1) and not RELU_S(t + 1):
-                    first_max(t + 1, True)
-                elif k == "r" and is_block(t + 1) and RELU_S(t + 1):
-                    first_max(t + 1, False)
-                elif k in "bc" and is_block(t + 1):
-                    running_max(t + 1, 2 + "bc".index(k))
-                elif k in "def":
-                    q = "def".index(k)
-                    if is_block(t):
-                        subtract_max(t, q + 1)
-                    n = 3 * t + q + ACC_BANKS
-                    if is_block(n // 3):
-                        mx_group(n // 3, n % 3 + 1)
-                elif k == "q" and qi is not None:
-                    quantise(qi)
-                elif k == "u":
-                    if left > 0:
-                        left -= 1
-                        next_unit()
-                elif k == "x" and x_turned < BLOCKS and x_turned == x_next and (t + 1 not in LN_STEP or (X_LN1 and t + 1 == LN_STEP[0])):
-                    transpose_x(x_turned, 0)
-                    x_turned += 1
-                elif k == "z" and xi is not None and not (PRE1 and t == 0):
-                    transpose_x(xi, 1)
-                elif k in "y" and xi is not None:
-                    transpose_x(xi, "yz".index(k))
-                elif k in "AB" and xi is not None:
-                    copy_x(xi, "AB".index(k), True)
-                elif k in "CD" and xi is not None:
-                    square_x(xi, "CD".index(k), True)
-                elif k in "YZ" and xi is not None:
-                    h = "YZ".index(k)
-                    if CPV(xi, h):
-                        copy_x(xi, h, True)
-                        square_x(xi, h, False)
-                    elif SQV(xi, h):
-                        copy_x(xi, h, False)
-                    else:
-                        copy_and_square(xi, h, XV(xi, h))
-                elif k in "VW" and qi is not None and qi >= READY:
-                    h = "VW".index(k)
-                    if SQV(qi, h):
-                        square_x(qi, h, True)
-                elif k == "E" and is_block(t - 1):
-                    exponentials(t - 1)
-                elif k == "G" and is_block(t - 1):
-                    sum_modes(t - 1)
-                elif k in "L!" and ln_group is not None and ln_next < LAST_OF[ln_group] + 1:
-                    for i in range(ln_next, LAST_OF[ln_group] + 1 if k == "L" else ln_next + 1):
-                        ln_next = i + 1
-                        ln_sum(i, "t%d" % (i % 2) if X_LN1 and ln_group == 0 else "xt%d" % (i % XT_BANKS))
-                    limit = LAST_OF[ln_group] + 1
-                elif k == "P":
-                    while state["recip"] < limit and 4 * state["recip"] < state["done"] + 2 * count + LOOK:
-                        reciprocal_sum(state["recip"])
-                        state["recip"] += 1
-            for n in range(left):
-                next_unit()
-            if t >= BLOCKS or t not in LN_STEP:
-                state["avail"] = 4 * state["recip"]
-            if t >= BLOCKS:
-                pump()
+            if t == BLOCKS - 1:
+                release_all(BLOCKS - 2)
+            turn_tiles()
+            if first_ln:
+                first_ln_step(t, x_block, q_block)
+            elif t == BLOCKS:
+                first_closing_step(t)
+            elif t > BLOCKS:
+                closing_step(t)
+            elif t in LN_STEPS:
+                ln_step(t, LN_STEPS.index(t), q_block)
+            else:
+                ordinary_step(t, x_block, q_block)
+            if t < BLOCKS - 1 and t not in LN_STEPS:
+                line["released"] = TILES_PER_BLOCK * line["divided"]
+            t += 1

from contextlib import ExitStack

import concourse.mybir as mybir
from concourse.masks import make_identity

F32 = mybir.dt.float32
BF16 = mybir.dt.bfloat16
U32 = mybir.dt.uint32
U8 = mybir.dt.uint8
FP8X4 = mybir.dt.float8_e4m3fn_x4
ALU = mybir.AluOpType
ACT = mybir.ActivationFunctionType

P = 128
SAMPLES = 8192
CLASSES = 128
MODES = 4
FEATURES = 512
PACK = 4
TILES = SAMPLES // P
TILES_PER_BLOCK = 4
BLOCKS = TILES // TILES_PER_BLOCK
BLOCK = TILES_PER_BLOCK * P
HALF = BLOCK // 2
FLOPS = 2 * 2 * SAMPLES * CLASSES * MODES * FEATURES

GAMMA_LOADS = 4
CLOSING_TILES = 8
X_BEFORE = 4
LN_GROUPS = (4, 4, 4, 2, 2)
FIRST_OF = [sum(LN_GROUPS[:g]) for g in range(len(LN_GROUPS))]
LAST_OF = [first + size - 1 for first, size in zip(FIRST_OF, LN_GROUPS)]
GROUP_OF = [g for g, size in enumerate(LN_GROUPS) for i in range(size)]
LN_STEPS = [last + 2 for last in LAST_OF]
FIRST_MAX_ON_VECTOR = set(range(8)) | {step + 1 for step in LN_STEPS}

GROUP_BANKS = ("p0", "p1", "p2", "p3")
X_BANKS = ("xt0", "xt1")
TILE_BANKS = ("t0", "t1")
WEIGHT_BANKS = ("t0", "t1", "p3", "p2")
WARM_BANK = "xt1"
WARM_PASSES = 4
CLOSING_WARM_BANK = "p2"
TENSOR_SUMS = {BLOCKS - 1}


def tile_dota_mix_pa_t_kernel(tc, x, gamma_class, mu, cur_var, pi, out):
    nc = tc.nc
    x_rows = x.rearrange("(p j) d -> p j d", j=TILES)
    gamma_rows = gamma_class.rearrange("(p j) k -> p j k", j=TILES)
    out_rows = out.rearrange("(p j) k m -> p j (k m)", j=TILES)

    with ExitStack() as ctx:
        ctx.enter_context(tc.manual_schedule())
        const = ctx.enter_context(tc.tile_pool(name="const", bufs=1))
        xin = ctx.enter_context(tc.tile_pool(name="xin", bufs=4))
        grp = ctx.enter_context(tc.tile_pool(name="grp", bufs=3))
        cod = ctx.enter_context(tc.tile_pool(name="cod", bufs=5))
        half = ctx.enter_context(tc.tile_pool(name="half", bufs=2))
        tops = ctx.enter_context(tc.tile_pool(name="tops", bufs=5))
        rat = ctx.enter_context(tc.tile_pool(name="rat", bufs=7))
        outp = ctx.enter_context(tc.tile_pool(name="outp", bufs=3))
        psum = ctx.enter_context(tc.psum_pool(name="psum", bufs=1))

        identity = const.tile([P, P], F32, name="identf")
        zeros = const.tile([P, BLOCK], BF16, name="zeros")
        identity_bf = const.tile([P, P], BF16, name="identb")
        w_words = const.tile([P, MODES, 2, CLASSES], U32, name="wq", align_bytes=64)
        w_scales = const.tile([P, MODES, 2, CLASSES], U8, name="ws", align_bytes=64)
        dbias = const.tile([P, MODES], F32, name="bd")
        gamma_sb = const.tile([P, TILES, CLASSES], BF16, name="g_sb")

        x_sb = {}
        x_t = {}
        grouped = {}
        operands = {}
        group_acc = {}
        top = {}
        expo = {}
        esum = {}
        sum_t = {}
        ratio = {}
        expo_t = {}
        result = {}

        def is_block(i):
            return 0 <= i < BLOCKS


        def load_x(i):
            x_sb[i] = xin.tile([P, TILES_PER_BLOCK, FEATURES], BF16, name="x_sb")
            nc.sync.dma_start(out=x_sb[i][:], in_=x_rows[:, i * TILES_PER_BLOCK : (i + 1) * TILES_PER_BLOCK, :])

        def load_gamma(c):
            js = slice(c * TILES // GAMMA_LOADS, (c + 1) * TILES // GAMMA_LOADS)
            nc.sync.dma_start(out=gamma_sb[:, js, :], in_=gamma_rows[:, js, :])

        def transpose_x(i, h):
            x_t[(i, h)] = psum.tile([P, 2, HALF], F32, tag=X_BANKS[h], name="xt")
            pairs = x_sb[i][:].bitcast(F32)
            for jj in range(2):
                for u in range(2):
                    nc.tensor.transpose(
                        x_t[(i, h)][:, u, jj * P : (jj + 1) * P], pairs[:, 2 * h + jj, u : 2 * P : 2], identity[:]
                    )

        def copy_x(i, h, on_vector):
            if i not in grouped:
                grouped[i] = grp.tile([P, 2, BLOCK, PACK], BF16, name="xg", align_bytes=64)
            dst = grouped[i][:, 1, h * HALF : (h + 1) * HALF, :].bitcast(F32)
            src = x_t[(i, h)][:].rearrange("p u c -> p c u")
            if on_vector:
                nc.vector.tensor_copy(out=dst, in_=src)
            else:
                nc.scalar.copy(out=dst, in_=src)

        def square_x(i, h, on_vector):
            xx_half = grouped[i][:, 0, h * HALF : (h + 1) * HALF, :]
            if on_vector:
                x_half = grouped[i][:, 1, h * HALF : (h + 1) * HALF, :].rearrange("p c t -> p (c t)")
                nc.vector.tensor_tensor(
                    out=xx_half.rearrange("p c t -> p (c t)"), in0=x_half, in1=x_half, op=ALU.mult
                )
            else:
                nc.scalar.activation(
                    out=xx_half.rearrange("p c (u e) -> p c u e", e=2),
                    in_=x_t[(i, h)][:].bitcast(BF16).rearrange("p u (c e) -> p c u e", e=2),
                    func=ACT.Square,
                )

        def copy_and_square(i, h):
            copy_x(i, h, False)
            square_x(i, h, False)

        def quantise_x(i):
            words = cod.tile([P, 2, BLOCK], U32, name="xq", align_bytes=64)
            scales = cod.tile([P, 2, BLOCK], U8, name="xs", align_bytes=64)
            operands[i] = (words, scales)
            nc.vector.quantize_mx(
                out=words[:].rearrange("p w c -> p (w c)").bitcast(FP8X4),
                scales=scales[:].rearrange("p w c -> p (w c)"),
                in_=grouped[i][:].rearrange("p w c t -> p (w c t)"),
            )


        def mx_group(n):
            i, m = n // 3, n % 3 + 1
            group_acc[(i, m)] = psum.tile([P, BLOCK], F32, tag=GROUP_BANKS[n % len(GROUP_BANKS)], name="acc")
            words, scales = operands[i]
            passes = ((0, m), (0, 0), (1, m), (1, 0))
            for s, (w, mode) in enumerate(passes):
                nc.tensor.matmul_mx(
                    out=group_acc[(i, m)][:],
                    lhsT=w_words[:, mode, w, :].bitcast(FP8X4),
                    lhsT_scale=w_scales[:, mode, w, :],
                    rhs=words[:, w, :].bitcast(FP8X4),
                    rhs_scale=scales[:, w, :],
                    start=(s == 0),
                    stop=(s == len(passes) - 1),
                )

        def first_max(i):
            top[i] = tops.tile([P, BLOCK], F32, name="top")
            if i in FIRST_MAX_ON_VECTOR:
                nc.vector.tensor_scalar(
                    out=top[i][:], in0=group_acc[(i, 1)][:], scalar1=dbias[:, 1:2], scalar2=0.0, op0=ALU.add, op1=ALU.max
                )
            else:
                nc.scalar.activation(out=top[i][:], in_=group_acc[(i, 1)][:], func=ACT.Relu, bias=dbias[:, 1:2])

        def running_max(i, m):
            if is_block(i):
                nc.vector.scalar_tensor_tensor(
                    out=top[i][:],
                    in0=group_acc[(i, m)][:],
                    scalar=dbias[:, m : m + 1],
                    in1=top[i][:],
                    op0=ALU.add,
                    op1=ALU.max,
                )

        def subtract_max(i, m):
            if is_block(i):
                if m == 1:
                    expo[i] = big.tile([P, MODES, BLOCK], F32, name="de")
                nc.vector.scalar_tensor_tensor(
                    out=expo[i][:, m, :],
                    in0=group_acc[(i, m)][:],
                    scalar=dbias[:, m : m + 1],
                    in1=top[i][:],
                    op0=ALU.add,
                    op1=ALU.subtract,
                )
            following = 3 * i + m - 1 + len(GROUP_BANKS)
            if is_block(following // 3):
                mx_group(following)
            elif is_block(i):
                bank = GROUP_BANKS[following % len(GROUP_BANKS)]
                if bank != CLOSING_WARM_BANK:
                    line["banks"] = line["banks"] + (bank,)
                    turn_tiles()

        def exponentials_and_sum(i):
            if is_block(i):
                nc.scalar.activation(out=expo[i][:, 0, :], in_=top[i][:], func=ACT.Exp, scale=-1.0)
                nc.scalar.activation(out=expo[i][:, 1:4, :], in_=expo[i][:, 1:4, :], func=ACT.Exp)
            if is_block(i) and i not in TENSOR_SUMS:
                half_sums = half.tile([P, 2, BLOCK], F32, name="hs")
                nc.gpsimd.tensor_tensor(
                    out=half_sums[:], in0=expo[i][:, 0:2, :], in1=expo[i][:, 2:4, :], op=ALU.add
                )
                g = GROUP_OF[i]
                if i == FIRST_OF[g]:
                    esum[g] = sums.tile([P, max(LN_GROUPS), BLOCK], F32, name="ssum")
                nc.gpsimd.tensor_tensor(
                    out=esum[g][:, i - FIRST_OF[g], :], in0=half_sums[:, 0, :], in1=half_sums[:, 1, :], op=ALU.add
                )


        def turn_sum(i, bank):
            sum_t[i] = psum.tile([P, TILES_PER_BLOCK, CLASSES], F32, tag=bank, name="st")
            g = GROUP_OF[i]
            for jl in range(TILES_PER_BLOCK):
                cols = slice(jl * P, (jl + 1) * P)
                terms = (
                    [expo[i][:, m, cols] for m in range(MODES)]
                    if i in TENSOR_SUMS
                    else [esum[g][:, i - FIRST_OF[g], cols]]
                )
                for n, term in enumerate(terms):
                    nc.tensor.matmul(
                        sum_t[i][:, jl, :],
                        lhsT=term,
                        rhs=identity[:],
                        start=(n == 0),
                        stop=(n == len(terms) - 1),
                        is_transpose=True,
                    )

        def ln_sum(i, bank):
            if i not in sum_t:
                turn_sum(i, bank)
            ratio[i] = rat.tile([P, TILES_PER_BLOCK, CLASSES], F32, name="rr")
            nc.scalar.activation(out=ratio[i][:], in_=sum_t[i][:], func=ACT.Ln)

        def warm(bank):
            unread = psum.tile([P, BLOCK], F32, tag=bank, name="scrap")
            nc.tensor.matmul(unread[:], lhsT=zeros[:, 0:P], rhs=zeros[:], start=True, stop=True)

        line = {"divided": 0, "released": 0, "turned": 0, "finished": 0, "banks": TILE_BANKS}
        bank_of = {}

        def divide_gamma(ln_blocks, per_step):
            while (
                line["divided"] < ln_blocks
                and TILES_PER_BLOCK * line["divided"] < line["finished"] + 2 * per_step + 2
            ):
                i = line["divided"]
                nc.scalar.activation(out=ratio[i][:], in_=ratio[i][:], func=ACT.Exp, scale=-1.0)
                js = slice(i * TILES_PER_BLOCK, (i + 1) * TILES_PER_BLOCK)
                nc.gpsimd.tensor_tensor(out=ratio[i][:], in0=ratio[i][:], in1=gamma_sb[:, js, :], op=ALU.mult)
                line["divided"] += 1

        def turn_tiles():
            while line["turned"] < line["released"] and line["banks"]:
                j = line["turned"]
                i, jl = divmod(j, TILES_PER_BLOCK)
                bank_of[j] = line["banks"][0]
                line["banks"] = line["banks"][1:]
                expo_t[j] = psum.tile([P, MODES, CLASSES], F32, tag=bank_of[j], name="tb")
                for m in range(MODES):
                    nc.tensor.transpose(expo_t[j][:, m, :], expo[i][:, m, jl * P : (jl + 1) * P], identity[:])
                line["turned"] += 1

        def finish_tile():
            j = line["finished"]
            if j == line["turned"]:
                return
            i, jl = divmod(j, TILES_PER_BLOCK)
            if jl == 0:
                result[i] = outp.tile([P, TILES_PER_BLOCK, CLASSES * MODES], F32, name="o_sb")
            parts = 2 if j == TILES - 1 else 1
            for c in range(parts):
                ks = slice(c * CLASSES // parts, (c + 1) * CLASSES // parts)
                cols = slice(c * CLASSES * MODES // parts, (c + 1) * CLASSES * MODES // parts)
                nc.vector.tensor_tensor(
                    out=result[i][:, jl, cols].rearrange("p (k m) -> p k m", m=MODES),
                    in0=expo_t[j][:, :, ks].rearrange("p m k -> p k m"),
                    in1=ratio[i][:, jl, ks].unsqueeze(2).to_broadcast([P, CLASSES // parts, MODES]),
                    op=ALU.mult,
                )
                nc.sync.dma_start(out=out_rows[:, j, cols], in_=result[i][:, jl, cols])
            line["banks"] = line["banks"] + (bank_of[j],)
            line["finished"] += 1
            turn_tiles()

        with tc.tile_pool(name="prep", bufs=1) as prep:
            var_sb = prep.tile([P, MODES, FEATURES], BF16, name="var_sb")
            mu_sb = prep.tile([P, MODES, FEATURES], BF16, name="mu_sb")
            pi_sb = prep.tile([P, MODES], BF16, name="pi_sb")
            nc.scalar.dma_start(out=pi_sb[:], in_=pi)
            for m in range(MODES):
                nc.sync.dma_start(out=var_sb[:, m, :], in_=cur_var[:, m, :])
            load_x(0)
            nc.sync.dma_start(out=mu_sb[:], in_=mu)
            for i in range(1, X_BEFORE):
                load_x(i)
            nc.vector.memset(zeros[:], 0.0)
            make_identity(nc, identity[:])
            nc.gpsimd.tensor_copy(out=identity_bf[:], in_=identity[:])

            ln_var = prep.tile([P, MODES, FEATURES], F32, name="lnv")
            inv_var = prep.tile([P, MODES, FEATURES], F32, name="ivp")
            mu_iv = prep.tile([P, MODES, FEATURES], F32, name="miv")
            w_rows = prep.tile([P, MODES, 2, FEATURES], BF16, name="wr", align_bytes=64)
            w_grouped = prep.tile([P, MODES, 2, CLASSES * PACK], BF16, name="wg", align_bytes=64)
            log_det = prep.tile([P, MODES], F32, name="ld")
            pi_eps = prep.tile([P, MODES], F32, name="pif")
            ln_pi = prep.tile([P, MODES], F32, name="lnpi")
            quad = prep.tile([P, MODES], F32, name="qs")
            bias = prep.tile([P, MODES], F32, name="bias")

            nc.gpsimd.tensor_scalar(out=pi_eps[:], in0=pi_sb[:], scalar1=1e-10, scalar2=0.0, op0=ALU.add, op1=ALU.add)
            for m in range(MODES):
                nc.scalar.activation(
                    out=ln_var[:, m, :], in_=var_sb[:, m, :], func=ACT.Ln, accum_out=log_det[:, m : m + 1]
                )
            nc.scalar.activation(out=ln_pi[:], in_=pi_eps[:], func=ACT.Ln)
            for m in range(MODES):
                nc.scalar.activation(out=inv_var[:, m, :], in_=ln_var[:, m, :], func=ACT.Exp, scale=-1.0)

            def sign(m):
                return -1.0 if m == 0 else 1.0

            def weigh(m):
                nc.vector.tensor_scalar(
                    out=w_rows[:, m, 0, :], in0=inv_var[:, m, :], scalar1=-0.5 * sign(m), scalar2=None, op0=ALU.mult
                )
                nc.vector.scalar_tensor_tensor(
                    out=mu_iv[:, m, :],
                    in0=mu_sb[:, m, :],
                    scalar=sign(m),
                    in1=inv_var[:, m, :],
                    op0=ALU.mult,
                    op1=ALU.mult,
                )

            def round_mu_iv(m):
                nc.vector.tensor_copy(out=w_rows[:, m, 1, :], in_=mu_iv[:, m, :])

            def turn_weights(m):
                w_t = psum.tile([P, 2, PACK, CLASSES], BF16, tag=WEIGHT_BANKS[m], name="wt")
                for w in range(2):
                    for t in range(PACK):
                        nc.tensor.transpose(w_t[:, w, t, :], w_rows[:, m, w, t::PACK], identity_bf[:])
                nc.scalar.copy(
                    out=w_grouped[:, m, :, :].rearrange("p w (k t) -> p w k t", t=PACK),
                    in_=w_t[:].rearrange("p w t k -> p w k t"),
                )

            def quantise_weights(m):
                nc.vector.quantize_mx(
                    out=w_words[:, m, :, :].rearrange("p w k -> p (w k)").bitcast(FP8X4),
                    scales=w_scales[:, m, :, :].rearrange("p w k -> p (w k)"),
                    in_=w_grouped[:, m, :, :].rearrange("p w k -> p (w k)"),
                )

            def sum_quad(m):
                nc.vector.scalar_tensor_tensor(
                    out=inv_var[:, m, :],
                    in0=mu_sb[:, m, :],
                    scalar=sign(m),
                    in1=mu_iv[:, m, :],
                    op0=ALU.mult,
                    op1=ALU.mult,
                    accum_out=quad[:, m : m + 1],
                )

            for n in range(WARM_PASSES):
                warm(WARM_BANK)

            for h in range(2):
                transpose_x(0, h)
                copy_x(0, h, True)
            load_x(X_BEFORE)
            transpose_x(1, 0)
            copy_and_square(1, 0)
            weigh(0)
            weigh(1)
            round_mu_iv(0)
            turn_weights(0)
            transpose_x(1, 1)
            weigh(2)
            round_mu_iv(1)
            turn_weights(1)
            transpose_x(2, 0)
            weigh(3)
            round_mu_iv(2)
            turn_weights(2)
            square_x(0, 0, True)
            round_mu_iv(3)
            turn_weights(3)
            square_x(0, 1, True)
            copy_and_square(1, 1)
            copy_and_square(2, 0)
            quantise_x(0)
            quantise_weights(0)
            quantise_weights(1)
            mx_group(0)
            quantise_weights(2)
            transpose_x(2, 1)
            mx_group(1)
            copy_and_square(2, 1)
            sum_quad(0)
            quantise_weights(3)
            transpose_x(3, 0)
            mx_group(2)
            copy_and_square(3, 0)
            sum_quad(1)
            quantise_x(1)
            sum_quad(2)
            sum_quad(3)
            nc.vector.tensor_tensor(out=quad[:], in0=quad[:], in1=log_det[:], op=ALU.add)
            nc.vector.scalar_tensor_tensor(
                out=bias[:], in0=quad[:], scalar=-0.5, in1=ln_pi[:], op0=ALU.mult, op1=ALU.add
            )
            nc.vector.tensor_scalar(out=dbias[:], in0=bias[:], scalar1=bias[:, 0:1], scalar2=None, op0=ALU.subtract)
            transpose_x(3, 1)
            mx_group(3)
            first_max(0)
            copy_and_square(3, 1)
            quantise_x(2)
            running_max(0, 2)
            running_max(0, 3)

        big = ctx.enter_context(tc.tile_pool(name="big", bufs=9))
        sums = ctx.enter_context(tc.tile_pool(name="sums", bufs=2))

        queue = {"loaded": X_BEFORE + 1, "prepared": X_BEFORE, "quantised": X_BEFORE - 1, "ln_blocks": 0}
        for h in range(2):
            transpose_x(X_BEFORE, h)

        def transpose_next_x(t):
            if is_block(queue["prepared"]) and (t + 1 not in LN_STEPS or t + 1 == LN_STEPS[0]):
                transpose_x(queue["prepared"], 0)

        def first_max_ahead(t, on_vector):
            if is_block(t + 1) and (t + 1 in FIRST_MAX_ON_VECTOR) == on_vector:
                first_max(t + 1)

        def ordinary_step(t, x_block, q_block):
            first_max_ahead(t, False)
            subtract_max(t, 1)
            finish_tile()
            if x_block is not None:
                copy_and_square(x_block, 0)
            first_max_ahead(t, True)
            finish_tile()
            if x_block is not None and x_block > X_BEFORE:
                transpose_x(x_block, 1)
            subtract_max(t, 2)
            running_max(t + 1, 2)
            exponentials_and_sum(t - 1)
            finish_tile()
            transpose_next_x(t)
            finish_tile()
            if q_block is not None:
                quantise_x(q_block)
            subtract_max(t, 3)
            running_max(t + 1, 3)
            if x_block is not None:
                copy_and_square(x_block, 1)
            divide_gamma(queue["ln_blocks"], TILES_PER_BLOCK)

        def first_ln_step(t, x_block, q_block):
            first_max_ahead(t, False)
            subtract_max(t, 1)
            transpose_x(x_block, 1)
            first_max_ahead(t, True)
            subtract_max(t, 2)
            copy_x(x_block, 0, True)
            running_max(t + 1, 2)
            copy_x(x_block, 1, True)
            quantise_x(q_block)
            exponentials_and_sum(t - 1)
            for i in range(FIRST_OF[0], LAST_OF[0] + 1):
                ln_sum(i, TILE_BANKS[i % 2])
            square_x(x_block, 0, True)
            subtract_max(t, 3)
            square_x(x_block, 1, True)
            running_max(t + 1, 3)
            transpose_next_x(t)
            queue["ln_blocks"] = LAST_OF[0] + 1
            divide_gamma(queue["ln_blocks"], TILES_PER_BLOCK)

        def ln_step(t, g, q_block):
            def next_ln_sum(k):
                i = FIRST_OF[g] + k
                if i <= LAST_OF[g]:
                    ln_sum(i, X_BANKS[i % 2])

            first_max_ahead(t, False)
            subtract_max(t, 1)
            first_max_ahead(t, True)
            exponentials_and_sum(t - 1)
            next_ln_sum(0)
            finish_tile()
            subtract_max(t, 2)
            next_ln_sum(1)
            running_max(t + 1, 2)
            next_ln_sum(2)
            finish_tile()
            if q_block is not None:
                quantise_x(q_block)
            next_ln_sum(3)
            subtract_max(t, 3)
            running_max(t + 1, 3)
            if t == BLOCKS - 1:
                for n in range(2):
                    warm(CLOSING_WARM_BANK)
            finish_tile()
            transpose_next_x(t)
            queue["ln_blocks"] = LAST_OF[g] + 1
            divide_gamma(queue["ln_blocks"], TILES_PER_BLOCK if t < BLOCKS - 1 else CLOSING_TILES)
            finish_tile()

        def warm_and_finish(n):
            for k in range(n):
                warm(CLOSING_WARM_BANK)
                finish_tile()

        def release_all(blocks):
            line["released"] = TILES_PER_BLOCK * blocks
            turn_tiles()

        def first_closing_step(t):
            warm_and_finish(2)
            exponentials_and_sum(t - 1)
            release_all(BLOCKS)
            warm_and_finish(3)
            turn_sum(BLOCKS - 2, X_BANKS[0])
            divide_gamma(queue["ln_blocks"], CLOSING_TILES)
            warm_and_finish(3)
            turn_sum(BLOCKS - 1, X_BANKS[1])

        def closing_step(t):
            if t in LN_STEPS:
                for i in range(FIRST_OF[-1], BLOCKS):
                    ln_sum(i, X_BANKS[i % 2])
                queue["ln_blocks"] = BLOCKS
            for n in range(3):
                finish_tile()
            divide_gamma(queue["ln_blocks"], CLOSING_TILES)
            for n in range(CLOSING_TILES - 3):
                finish_tile()

        t = 0
        while line["finished"] < TILES:
            first_ln = t == LN_STEPS[0]
            x_block = None
            q_block = None
            if queue["quantised"] < min(queue["prepared"], BLOCKS):
                q_block = queue["quantised"]
                queue["quantised"] += 1
            if first_ln or t not in LN_STEPS:
                if is_block(queue["prepared"]):
                    x_block = queue["prepared"]
                queue["prepared"] += 1
            if is_block(queue["loaded"]) and queue["loaded"] <= queue["prepared"] + 1:
                load_x(queue["loaded"])
                queue["loaded"] += 1
            if t < GAMMA_LOADS:
                load_gamma(t)
            if t == BLOCKS - 1:
                release_all(BLOCKS - 2)
            turn_tiles()
            if first_ln:
                first_ln_step(t, x_block, q_block)
            elif t == BLOCKS:
                first_closing_step(t)
            elif t > BLOCKS:
                closing_step(t)
            elif t in LN_STEPS:
                ln_step(t, LN_STEPS.index(t), q_block)
            else:
                ordinary_step(t, x_block, q_block)
            if t < BLOCKS - 1 and t not in LN_STEPS:
                line["released"] = TILES_PER_BLOCK * line["divided"]
            t += 1
